import numpy as np
import ml_dtypes


def mxq(x, axis, fmt="e4m3"):
    dtype, down = {"e4m3": (ml_dtypes.float8_e4m3fn, 7), "e5m2": (ml_dtypes.float8_e5m2, 14)}[fmt]
    v = np.moveaxis(np.asarray(x, np.float32).astype(ml_dtypes.bfloat16).astype(np.float64), axis, -1)
    blocks = v.reshape(v.shape[:-1] + (-1, 32))
    amax = np.abs(blocks).max(-1, keepdims=True)
    byte = np.maximum(np.where(amax > 0, np.frexp(amax)[1] - 1 + 127, 0) - down, 1)
    scale = np.exp2(byte - 127.0)
    codes = (blocks / scale).astype(np.float32).astype(dtype).astype(np.float64)
    return np.moveaxis((codes * scale).reshape(v.shape), -1, axis)


WIDE = False


def mx_kscale(k):
    if not WIDE:
        return np.ones(k)
    levels = np.array([10, -10, 5, -5, 0])
    a = np.random.permutation(np.resize(levels, k // 512 * 4)).reshape(k // 512, 4)
    idx = np.arange(k)
    return np.exp2(a[idx // 512, idx % 128 // 32])


BF16 = ml_dtypes.bfloat16


def bf(x):
    return np.asarray(x, np.float32).astype(BF16)


def f64(x):
    return np.asarray(x).astype(np.float64)


E2M1 = np.array([0.0, 0.5, 1.0, 1.5, 2.0, 3.0, 4.0, 6.0, -0.0, -0.5, -1.0, -1.5, -2.0, -3.0, -4.0, -6.0])


def pack_weight(w, fmt):
    k, n = w.shape
    w = f64(bf(w)).reshape(k // 32, 32, n)
    amax = np.abs(w).max(1)
    if fmt == "e4m3":
        byte = np.frexp(amax)[1] - 1 + 127 - 7
    else:
        mant, ex = np.frexp(amax / 6.0)
        byte = np.where(mant > 0.5, ex, ex - 1) + 127
    byte = np.clip(np.where(amax > 0, byte, 1), 1, 254)
    scaled = (w * np.exp2(127.0 - byte)[:, None, :]).reshape(k, n).astype(np.float32)
    by_word = np.ascontiguousarray(scaled.reshape(k // 512, 128, 4, n).transpose(0, 1, 3, 2))
    if fmt == "e4m3":
        words = by_word.astype(ml_dtypes.float8_e4m3fn).view(np.uint8)
    else:
        c = by_word.astype(ml_dtypes.float4_e2m1fn).view(np.uint8) & 0xF
        words = c[..., 0::2] | (c[..., 1::2] << 4)
    return np.ascontiguousarray(words), np.ascontiguousarray(byte.astype(np.uint8).reshape(k // 512, 16, n))


def unpack_weight(words, scales, fmt):
    g, p, n, _ = words.shape
    if fmt == "e4m3":
        vals = np.ascontiguousarray(words).view(ml_dtypes.float8_e4m3fn).astype(np.float64)
    else:
        nib = np.empty((g, p, n, 4), np.uint8)
        nib[..., 0::2] = words & 0xF
        nib[..., 1::2] = words >> 4
        vals = E2M1[nib]
    vals = vals * np.repeat(np.exp2(scales.astype(np.float64) - 127.0), 8, axis=1)[..., None]
    return vals.transpose(0, 1, 3, 2).reshape(g * 512, n)


B, H, W, D, Dh, Dq, R, T = 16, 16, 16, 512, 512, 128, 16, 8
EPS = 1e-6
FMT = "e4m3"


def layer_norm(v, g, b):
    mu = v.mean(-1, keepdims=True)
    var = ((v - mu) ** 2).mean(-1, keepdims=True)
    return (v - mu) / np.sqrt(var + EPS) * g + b


def setup_inputs():
    rn = np.random.standard_normal
    s, t = mx_kscale(D), mx_kscale(Dh)
    x = bf(rn((B, H, W, D)) * s)
    z2 = bf(rn((B, H, W, Dq)) * 1.5)
    U1_w_words, U1_w_scales = pack_weight(np.ascontiguousarray((rn((Dh, D)) * np.sqrt(2.0 / D) / s).T), FMT)
    U1_b = bf(rn(Dh) * 0.5)
    U3_w = bf(rn((Dh, Dq)) * np.sqrt(2.0 / Dq))
    U3_b = bf(rn(Dh) * 0.5)
    C_w_words, C_w_scales = pack_weight(np.ascontiguousarray((rn((D, Dh)) / np.sqrt(Dh) / t).T), FMT)
    return {
        "x": x,
        "z2": z2,
        "U1_w_words": U1_w_words,
        "U1_w_scales": U1_w_scales,
        "U1_b": U1_b,
        "U3_w": U3_w,
        "U3_b": U3_b,
        "C_w_words": C_w_words,
        "C_w_scales": C_w_scales,
        "C_b": bf(rn(D) * 0.3),
        "ln1_g": bf((1.0 + 0.1 * rn(Dh)) * t),
        "ln1_b": bf(0.2 * rn(Dh) * t),
        "ln3_g": bf(1.0 + 0.1 * rn(Dh)),
        "ln3_b": bf(0.2 * rn(Dh)),
        "alpha": bf(0.6 + 0.2 * np.random.random(1)),
    }


def reference(x, z2, U1_w_words, U1_w_scales, U1_b, U3_w, U3_b, C_w_words, C_w_scales, C_b, ln1_g, ln1_b, ln3_g, ln3_b, alpha):
    out1 = (mxq(f64(x), 3, "e4m3") @ unpack_weight(U1_w_words, U1_w_scales, FMT)) + f64(U1_b)
    out3 = f64(z2) @ f64(U3_w).T + f64(U3_b)
    o1 = layer_norm(out1, f64(ln1_g), f64(ln1_b))
    o3 = layer_norm(out3, f64(ln3_g), f64(ln3_b))
    h = o1 + f64(alpha) * (o1 * o3)
    return (mxq(h, 3, "e4m3") @ unpack_weight(C_w_words, C_w_scales, FMT)) + f64(C_b)

@@ -1,0 +1,359 @@
+from contextlib import ExitStack
+
+import concourse.mybir as mybir
+from concourse.masks import make_identity
+
+F32 = mybir.dt.float32
+BF16 = mybir.dt.bfloat16
+I32 = mybir.dt.int32
+U32 = mybir.dt.uint32
+U8 = mybir.dt.uint8
+FP8X4 = mybir.dt.float8_e4m3fn_x4
+ALU = mybir.AluOpType
+ACT = mybir.ActivationFunctionType
+
+P = 128
+PACK = 4
+TOKENS = 16 * 16 * 16
+D = 512
+DQ = 128
+EPS = 1e-6
+TILES = TOKENS // P
+GROUP = 2
+X_CHUNK = 4
+
+FLOPS = 2 * TOKENS * D * D * 2 + 2 * TOKENS * DQ * D
+
+
+def load_mx_weight(nc, pool, words, scales, name):
+    codes = pool.tile([P, PACK * D], U8, name=name + "_codes", align_bytes=64)
+    plane = pool.tile([P, D], U8, name=name + "_plane", align_bytes=64)
+    nc.vector.memset(plane[:].bitcast(I32), 0)
+    for quadrant in range(4):
+        nc.sync.dma_start(
+            out=plane[32 * quadrant : 32 * quadrant + 4, :].bitcast(I32),
+            in_=scales[0, 4 * quadrant : 4 * quadrant + 4, :].bitcast(I32),
+        )
+    nc.sync.dma_start(
+        out=codes[:].bitcast(I32),
+        in_=words[0].rearrange("p n t -> p (n t)").bitcast(I32),
+    )
+    return codes, plane
+
+
+def tile_polymlp_skiplora_pa_t_kernel(
+    tc,
+    x,
+    z2,
+    U1_w_words,
+    U1_w_scales,
+    U1_b,
+    U3_w,
+    U3_b,
+    C_w_words,
+    C_w_scales,
+    C_b,
+    ln1_g,
+    ln1_b,
+    ln3_g,
+    ln3_b,
+    alpha,
+    out,
+):
+    nc = tc.nc
+    x_view = x.flatten_outer_dims().rearrange("(p i) d -> p i d", i=TILES)
+    z_view = z2.flatten_outer_dims().rearrange("(p i) d -> p i d", i=TILES)
+    out_view = out.flatten_outer_dims().rearrange("(p i) d -> p i d", i=TILES)
+
+    with ExitStack() as ctx:
+        consts = ctx.enter_context(tc.tile_pool(name="consts", bufs=1))
+        keep = ctx.enter_context(tc.tile_pool(name="keep", bufs=1))
+        x_in = ctx.enter_context(tc.tile_pool(name="x_in", bufs=TILES // X_CHUNK))
+        stage = ctx.enter_context(tc.tile_pool(name="stage", bufs=2))
+        pre_pool = ctx.enter_context(tc.tile_pool(name="pre_pool", bufs=3))
+        small = ctx.enter_context(tc.tile_pool(name="small", bufs=4))
+        results = ctx.enter_context(tc.tile_pool(name="results", bufs=3))
+        psum_first = ctx.enter_context(tc.psum_pool(name="psum_first", bufs=2 * GROUP))
+        psum_last = ctx.enter_context(tc.psum_pool(name="psum_last", bufs=GROUP))
+        psum_tr = ctx.enter_context(tc.psum_pool(name="psum_tr", bufs=2))
+        ctx.enter_context(tc.manual_schedule())
+
+        eps = consts.tile([P, 1], F32)
+        nc.vector.memset(eps[:], EPS)
+        table_warm = consts.tile([P, 1], F32)
+        nc.scalar.activation(out=table_warm[:], in_=eps[:], func=ACT.Sqrt)
+
+        ident_f32 = consts.tile([P, P], F32)
+        make_identity(nc, ident_f32[:])
+        ident_bf16 = consts.tile([P, P], BF16)
+        make_identity(nc, ident_bf16[:])
+
+        x_chunks = []
+        z_chunks = []
+        for c in range(TILES // X_CHUNK):
+            x_chunk = x_in.tile([P, X_CHUNK, D], BF16)
+            nc.sync.dma_start(out=x_chunk[:], in_=x_view[:, X_CHUNK * c : X_CHUNK * (c + 1), :])
+            x_chunks.append(x_chunk)
+            z_chunk = x_in.tile([P, X_CHUNK, DQ], BF16)
+            nc.sync.dma_start(out=z_chunk[:], in_=z_view[:, X_CHUNK * c : X_CHUNK * (c + 1), :])
+            z_chunks.append(z_chunk)
+            if c == 0:
+                w1_codes, w1_plane = load_mx_weight(nc, consts, U1_w_words, U1_w_scales, "w1")
+        c_codes, c_plane = load_mx_weight(nc, consts, C_w_words, C_w_scales, "c")
+
+        u3_rows = consts.tile([P, PACK, DQ], BF16)
+        nc.scalar.dma_start(out=u3_rows[:], in_=U3_w.rearrange("(m t) k -> m t k", t=PACK))
+
+        def broadcast_row(vec, name):
+            row = consts.tile([P, D], BF16, name=name)
+            nc.scalar.dma_start(out=row[:], in_=vec.partition_broadcast(P))
+            return row
+
+        u1_b_row = broadcast_row(U1_b, "u1_b_row")
+        u3_b_row = broadcast_row(U3_b, "u3_b_row")
+
+        def load_by_feature(vec, name):
+            column = consts.tile([P, PACK], BF16, name=name)
+            nc.scalar.dma_start(out=column[:], in_=vec.rearrange("(m t) -> m t", t=PACK))
+            return column
+
+        with nc.allow_non_contiguous_dma(reason="four neighbouring elements of a 512-vector to a partition"):
+            g1_raw = load_by_feature(ln1_g, "g1_raw")
+            b1_raw = load_by_feature(ln1_b, "b1_raw")
+            g3_raw = load_by_feature(ln3_g, "g3_raw")
+            b3_raw = load_by_feature(ln3_b, "b3_raw")
+            alpha_raw = consts.tile([P, 1], BF16)
+            nc.scalar.dma_start(out=alpha_raw[:], in_=alpha.partition_broadcast(P))
+        c_b_row = broadcast_row(C_b, "c_b_row")
+
+        xq_codes = keep.tile([P, TOKENS], U32, align_bytes=64)
+        xq_plane = keep.tile([P, TOKENS], U8, align_bytes=64)
+        z2T = keep.tile([P, TOKENS], BF16)
+
+        for c in range(TILES // X_CHUNK):
+            x_words = x_chunks[c][:].rearrange("p i d -> p (i d)").bitcast(F32)
+            words_per_tile = D // 2
+            x_grouped = stage.tile([P, X_CHUNK * P, PACK], BF16, align_bytes=64)
+            grouped_words = x_grouped[:].rearrange("p w t -> p (w t)").bitcast(F32)
+            for half in range(X_CHUNK // 2):
+                xT_bank = psum_first.tile([P, 2, 2, P], F32, tag="first")
+                for i in range(2):
+                    first = words_per_tile * (2 * half + i)
+                    for u in range(2):
+                        nc.tensor.transpose(
+                            xT_bank[:, i, u, :],
+                            x_words[:, first + u : first + words_per_tile : 2],
+                            ident_f32[:],
+                        )
+                nc.scalar.copy(
+                    out=grouped_words[:, 4 * P * half : 4 * P * (half + 1)].rearrange(
+                        "p (i w u) -> p i w u", i=2, u=2
+                    ),
+                    in_=xT_bank[:].rearrange("p i u w -> p i w u"),
+                )
+            zT_bank = psum_last.tile([P, X_CHUNK, P], BF16, tag="last")
+            for i in range(X_CHUNK):
+                nc.tensor.transpose(zT_bank[:, i, :], z_chunks[c][:, i, :], ident_bf16[:])
+            chunk_cols = slice(X_CHUNK * P * c, X_CHUNK * P * (c + 1))
+            nc.vector.tensor_copy(out=z2T[:, chunk_cols], in_=zT_bank[:].rearrange("p i w -> p (i w)"))
+            nc.vector.quantize_mx(
+                out=xq_codes[:, chunk_cols].bitcast(FP8X4),
+                scales=xq_plane[:, chunk_cols],
+                in_=x_grouped[:].rearrange("p w t -> p (w t)"),
+            )
+
+        u3T_bank = psum_tr.tile([P, PACK, P], BF16, tag="tr")
+        for t in range(PACK):
+            nc.tensor.transpose(u3T_bank[:, t, :], u3_rows[:, t, :], ident_bf16[:])
+        u3T = consts.tile([P, PACK, P], BF16)
+        nc.vector.tensor_copy(out=u3T[:], in_=u3T_bank[:])
+
+        bias1 = consts.tile([P, PACK, P], F32)
+        nc.vector.tensor_copy(out=bias1[:], in_=u1_b_row[:].rearrange("p (m t) -> p t m", t=PACK))
+        bias3 = consts.tile([P, PACK, P], F32)
+        nc.vector.tensor_copy(out=bias3[:], in_=u3_b_row[:].rearrange("p (m t) -> p t m", t=PACK))
+        bias_out = consts.tile([P, D], F32)
+        nc.vector.tensor_copy(out=bias_out[:], in_=c_b_row[:])
+
+        alpha_f32 = consts.tile([P, 1], F32)
+        nc.vector.tensor_copy(out=alpha_f32[:], in_=alpha_raw[:])
+        gain1 = consts.tile([P, PACK], F32)
+        nc.vector.tensor_copy(out=gain1[:], in_=g1_raw[:])
+        shift1 = consts.tile([P, PACK], F32)
+        nc.vector.tensor_copy(out=shift1[:], in_=b1_raw[:])
+        gain3 = consts.tile([P, PACK], F32)
+        nc.vector.tensor_scalar(
+            out=gain3[:], in0=g3_raw[:], scalar1=alpha_f32[:, 0:1], scalar2=None, op0=ALU.mult
+        )
+        shift3 = consts.tile([P, PACK], F32)
+        nc.vector.tensor_scalar(
+            out=shift3[:], in0=b3_raw[:], scalar1=alpha_f32[:, 0:1], scalar2=1.0, op0=ALU.mult, op1=ALU.add
+        )
+        gains = [gain1, gain3]
+        shifts = [shift1, shift3]
+        biases = [bias1, bias3]
+
+        live = {}
+
+        def first_matmuls(g):
+            y1 = pre_pool.tile([P, GROUP, PACK, P], F32)
+            y3 = pre_pool.tile([P, GROUP, PACK, P], F32)
+            pre_norm = [y1, y3]
+            sums = small.tile([P, 2, GROUP], F32)
+            by_feature_tile = []
+            for j in range(GROUP):
+                cols = slice(P * (GROUP * g + j), P * (GROUP * g + j + 1))
+                acc1 = psum_first.tile([P, D], F32, tag="first")
+                nc.tensor.matmul_mx(
+                    out=acc1[:],
+                    lhsT=xq_codes[:, cols].bitcast(FP8X4),
+                    lhsT_scale=xq_plane[:, cols],
+                    rhs=w1_codes[:].bitcast(FP8X4),
+                    rhs_scale=w1_plane[:],
+                    start=True,
+                    stop=True,
+                )
+                acc3 = psum_first.tile([P, D], F32, tag="first")
+                nc.tensor.matmul(
+                    out=acc3[:],
+                    lhsT=z2T[:, cols],
+                    rhs=u3T[:].rearrange("k t m -> k (t m)"),
+                    start=True,
+                    stop=True,
+                )
+                by_feature_tile.append(
+                    [
+                        acc1[:].rearrange("p (m t) -> p t m", t=PACK),
+                        acc3[:].rearrange("p (t m) -> p t m", t=PACK),
+                    ]
+                )
+            for j in range(GROUP):
+                for branch in range(2):
+                    nc.vector.scalar_tensor_tensor(
+                        out=pre_norm[branch][:, j, :, :],
+                        in0=by_feature_tile[j][branch],
+                        scalar=1.0,
+                        in1=biases[branch][:],
+                        op0=ALU.mult,
+                        op1=ALU.add,
+                        accum_out=sums[:, branch, j : j + 1],
+                    )
+            neg_mean = small.tile([P, 2, GROUP], F32)
+            nc.vector.tensor_scalar(
+                out=neg_mean[:], in0=sums[:], scalar1=-1.0 / D, scalar2=None, op0=ALU.mult
+            )
+            live[g] = {"pre_norm": pre_norm, "neg_mean": neg_mean}
+
+        def deviations(g):
+            square_sums = small.tile([P, 2, GROUP], F32)
+            for branch in range(2):
+                for j in range(GROUP):
+                    squares = stage.tile([P, D], F32)
+                    nc.scalar.activation(
+                        out=squares[:],
+                        in_=live[g]["pre_norm"][branch][:, j, :, :].rearrange("p t m -> p (t m)"),
+                        func=ACT.Square,
+                        bias=live[g]["neg_mean"][:, branch, j : j + 1],
+                        scale=1.0,
+                        accum_out=square_sums[:, branch, j : j + 1],
+                    )
+            std = small.tile([P, 2, GROUP], F32)
+            nc.scalar.activation(
+                out=std[:], in_=square_sums[:], func=ACT.Sqrt, bias=eps[:, 0:1], scale=1.0 / D
+            )
+            live[g]["std"] = std
+
+        def normalise(g):
+            rstd = small.tile([P, 2, GROUP], F32)
+            nc.vector.reciprocal(out=rstd[:], in_=live[g]["std"][:])
+            n1 = stage.tile([P, GROUP, PACK, P], F32)
+            n3 = stage.tile([P, GROUP, PACK, P], F32)
+            normed = [n1, n3]
+            for branch in range(2):
+                for j in range(GROUP):
+                    nc.gpsimd.tensor_scalar(
+                        out=normed[branch][:, j, :, :],
+                        in0=live[g]["pre_norm"][branch][:, j, :, :],
+                        scalar1=live[g]["neg_mean"][:, branch, j : j + 1],
+                        scalar2=rstd[:, branch, j : j + 1],
+                        op0=ALU.add,
+                        op1=ALU.mult,
+                    )
+            live[g]["normed"] = normed
+
+        def to_features(g):
+            o1T = stage.tile([P, PACK, GROUP * P], F32)
+            o3T = stage.tile([P, PACK, GROUP * P], F32)
+            scaled = [o1T, o3T]
+            for branch in range(2):
+                for pair in range(PACK // 2):
+                    nT_bank = psum_tr.tile([P, 2, GROUP * P], F32, tag="tr")
+                    for s in range(2):
+                        for j in range(GROUP):
+                            nc.tensor.transpose(
+                                nT_bank[:, s, P * j : P * (j + 1)],
+                                live[g]["normed"][branch][:, j, 2 * pair + s, :],
+                                ident_f32[:],
+                            )
+                    for s in range(2):
+                        t = 2 * pair + s
+                        nc.scalar.activation(
+                            out=scaled[branch][:, t, :],
+                            in_=nT_bank[:, s, :],
+                            func=ACT.Identity,
+                            bias=shifts[branch][:, t : t + 1],
+                            scale=gains[branch][:, t : t + 1],
+                        )
+            live[g]["scaled"] = scaled
+
+        def gate_and_quantise(g):
+            o1T, o3T = live[g]["scaled"]
+            h_grouped = stage.tile([P, GROUP * P, PACK], BF16, align_bytes=64)
+            nc.vector.tensor_tensor(
+                out=h_grouped[:].rearrange("p (c i) t -> p c t i", i=4),
+                in0=o1T[:].rearrange("p t (c i) -> p c t i", i=4),
+                in1=o3T[:].rearrange("p t (c i) -> p c t i", i=4),
+                op=ALU.mult,
+            )
+            hq_codes = stage.tile([P, GROUP * P], U32, align_bytes=64)
+            hq_plane = stage.tile([P, GROUP * P], U8, align_bytes=64)
+            nc.vector.quantize_mx(
+                out=hq_codes[:].bitcast(FP8X4),
+                scales=hq_plane[:],
+                in_=h_grouped[:].rearrange("p w t -> p (w t)"),
+            )
+            live[g]["hq"] = (hq_codes, hq_plane)
+
+        def last_matmul(g):
+            hq_codes, hq_plane = live[g]["hq"]
+            result = results.tile([P, GROUP, D], F32)
+            banks = []
+            for j in range(GROUP):
+                acc_out = psum_last.tile([P, D], F32, tag="last")
+                nc.tensor.matmul_mx(
+                    out=acc_out[:],
+                    lhsT=hq_codes[:, P * j : P * (j + 1)].bitcast(FP8X4),
+                    lhsT_scale=hq_plane[:, P * j : P * (j + 1)],
+                    rhs=c_codes[:].bitcast(FP8X4),
+                    rhs_scale=c_plane[:],
+                    start=True,
+                    stop=True,
+                )
+                banks.append(acc_out)
+            for j in range(GROUP):
+                nc.vector.tensor_tensor(out=result[:, j, :], in0=banks[j][:], in1=bias_out[:], op=ALU.add)
+            nc.sync.dma_start(out=out_view[:, GROUP * g : GROUP * (g + 1), :], in_=result[:])
+
+        groups = TILES // GROUP
+        for k in range(groups + 3):
+            if 0 <= k - 3 < groups:
+                gate_and_quantise(k - 3)
+            if k < groups:
+                first_matmuls(k)
+            if 0 <= k - 3 < groups:
+                last_matmul(k - 3)
+            if 0 <= k - 1 < groups:
+                deviations(k - 1)
+                normalise(k - 1)
+            if 0 <= k - 2 < groups:
+                to_features(k - 2)

@@ -21,6 +21,8 @@ EPS = 1e-6
 TILES = TOKENS // P
 GROUP = 2
 X_CHUNK = 4
+CHUNKS = TILES // X_CHUNK
+GROUPS = TILES // GROUP
 
 FLOPS = 2 * TOKENS * D * D * 2 + 2 * TOKENS * DQ * D
 
@@ -68,14 +70,13 @@ def tile_polymlp_skiplora_pa_t_kernel(
     with ExitStack() as ctx:
         consts = ctx.enter_context(tc.tile_pool(name="consts", bufs=1))
         keep = ctx.enter_context(tc.tile_pool(name="keep", bufs=1))
-        x_in = ctx.enter_context(tc.tile_pool(name="x_in", bufs=TILES // X_CHUNK))
+        x_in = ctx.enter_context(tc.tile_pool(name="x_in", bufs=CHUNKS))
         stage = ctx.enter_context(tc.tile_pool(name="stage", bufs=2))
-        pre_pool = ctx.enter_context(tc.tile_pool(name="pre_pool", bufs=3))
-        small = ctx.enter_context(tc.tile_pool(name="small", bufs=4))
+        pre_pool = ctx.enter_context(tc.tile_pool(name="pre_pool", bufs=4))
+        small = ctx.enter_context(tc.tile_pool(name="small", bufs=5))
         results = ctx.enter_context(tc.tile_pool(name="results", bufs=3))
-        psum_first = ctx.enter_context(tc.psum_pool(name="psum_first", bufs=2 * GROUP))
         psum_last = ctx.enter_context(tc.psum_pool(name="psum_last", bufs=GROUP))
-        psum_tr = ctx.enter_context(tc.psum_pool(name="psum_tr", bufs=2))
+        psum_turn = ctx.enter_context(tc.psum_pool(name="psum_turn", bufs=8 - GROUP))
         ctx.enter_context(tc.manual_schedule())
 
         eps = consts.tile([P, 1], F32)
@@ -90,7 +91,7 @@ def tile_polymlp_skiplora_pa_t_kernel(
 
         x_chunks = []
         z_chunks = []
-        for c in range(TILES // X_CHUNK):
+        for c in range(CHUNKS):
             x_chunk = x_in.tile([P, X_CHUNK, D], BF16)
             nc.sync.dma_start(out=x_chunk[:], in_=x_view[:, X_CHUNK * c : X_CHUNK * (c + 1), :])
             x_chunks.append(x_chunk)
@@ -104,13 +105,12 @@ def tile_polymlp_skiplora_pa_t_kernel(
         u3_rows = consts.tile([P, PACK, DQ], BF16)
         nc.scalar.dma_start(out=u3_rows[:], in_=U3_w.rearrange("(m t) k -> m t k", t=PACK))
 
-        def broadcast_row(vec, name):
-            row = consts.tile([P, D], BF16, name=name)
-            nc.scalar.dma_start(out=row[:], in_=vec.partition_broadcast(P))
-            return row
-
-        u1_b_row = broadcast_row(U1_b, "u1_b_row")
-        u3_b_row = broadcast_row(U3_b, "u3_b_row")
+        bias_rows = consts.tile([P, 3, D], BF16)
+        nc.vector.memset(bias_rows[:], 0.0)
+        for v, vec in enumerate([U1_b, U3_b, C_b]):
+            nc.scalar.dma_start(out=bias_rows[0:1, v, :], in_=vec.unsqueeze(0))
+        ones = consts.tile([P, P], BF16)
+        nc.vector.memset(ones[:], 1.0)
 
         def load_by_feature(vec, name):
             column = consts.tile([P, PACK], BF16, name=name)
@@ -124,19 +124,22 @@ def tile_polymlp_skiplora_pa_t_kernel(
             b3_raw = load_by_feature(ln3_b, "b3_raw")
             alpha_raw = consts.tile([P, 1], BF16)
             nc.scalar.dma_start(out=alpha_raw[:], in_=alpha.partition_broadcast(P))
-        c_b_row = broadcast_row(C_b, "c_b_row")
 
         xq_codes = keep.tile([P, TOKENS], U32, align_bytes=64)
         xq_plane = keep.tile([P, TOKENS], U8, align_bytes=64)
         z2T = keep.tile([P, TOKENS], BF16)
+        grouped_x = {}
 
-        for c in range(TILES // X_CHUNK):
+        def chunk_columns(c):
+            return slice(X_CHUNK * P * c, X_CHUNK * P * (c + 1))
+
+        def unpack(c):
             x_words = x_chunks[c][:].rearrange("p i d -> p (i d)").bitcast(F32)
             words_per_tile = D // 2
             x_grouped = stage.tile([P, X_CHUNK * P, PACK], BF16, align_bytes=64)
             grouped_words = x_grouped[:].rearrange("p w t -> p (w t)").bitcast(F32)
             for half in range(X_CHUNK // 2):
-                xT_bank = psum_first.tile([P, 2, 2, P], F32, tag="first")
+                xT_bank = psum_turn.tile([P, 2, 2, P], F32, tag="turn")
                 for i in range(2):
                     first = words_per_tile * (2 * half + i)
                     for u in range(2):
@@ -151,42 +154,50 @@ def tile_polymlp_skiplora_pa_t_kernel(
                     ),
                     in_=xT_bank[:].rearrange("p i u w -> p i w u"),
                 )
+            grouped_x[c] = x_grouped
             zT_bank = psum_last.tile([P, X_CHUNK, P], BF16, tag="last")
             for i in range(X_CHUNK):
                 nc.tensor.transpose(zT_bank[:, i, :], z_chunks[c][:, i, :], ident_bf16[:])
-            chunk_cols = slice(X_CHUNK * P * c, X_CHUNK * P * (c + 1))
-            nc.vector.tensor_copy(out=z2T[:, chunk_cols], in_=zT_bank[:].rearrange("p i w -> p (i w)"))
+            nc.scalar.copy(out=z2T[:, chunk_columns(c)], in_=zT_bank[:].rearrange("p i w -> p (i w)"))
+
+        def quantise_x(c):
             nc.vector.quantize_mx(
-                out=xq_codes[:, chunk_cols].bitcast(FP8X4),
-                scales=xq_plane[:, chunk_cols],
-                in_=x_grouped[:].rearrange("p w t -> p (w t)"),
+                out=xq_codes[:, chunk_columns(c)].bitcast(FP8X4),
+                scales=xq_plane[:, chunk_columns(c)],
+                in_=grouped_x[c][:].rearrange("p w t -> p (w t)"),
             )
 
-        u3T_bank = psum_tr.tile([P, PACK, P], BF16, tag="tr")
+        u3T_bank = psum_last.tile([P, PACK, P], BF16, tag="last")
         for t in range(PACK):
             nc.tensor.transpose(u3T_bank[:, t, :], u3_rows[:, t, :], ident_bf16[:])
         u3T = consts.tile([P, PACK, P], BF16)
         nc.vector.tensor_copy(out=u3T[:], in_=u3T_bank[:])
 
         bias1 = consts.tile([P, PACK, P], F32)
-        nc.vector.tensor_copy(out=bias1[:], in_=u1_b_row[:].rearrange("p (m t) -> p t m", t=PACK))
         bias3 = consts.tile([P, PACK, P], F32)
-        nc.vector.tensor_copy(out=bias3[:], in_=u3_b_row[:].rearrange("p (m t) -> p t m", t=PACK))
         bias_out = consts.tile([P, D], F32)
-        nc.vector.tensor_copy(out=bias_out[:], in_=c_b_row[:])
+        for v, spread in enumerate([bias1, bias3, bias_out]):
+            bias_bank = psum_turn.tile([P, D], F32, tag="turn")
+            nc.tensor.matmul(out=bias_bank[:], lhsT=ones[:], rhs=bias_rows[:, v, :], start=True, stop=True)
+            if v < 2:
+                nc.vector.tensor_copy(out=spread[:], in_=bias_bank[:].rearrange("p (m t) -> p t m", t=PACK))
+            else:
+                nc.vector.tensor_copy(out=spread[:], in_=bias_bank[:])
+
+        unpack(0)
 
         alpha_f32 = consts.tile([P, 1], F32)
-        nc.vector.tensor_copy(out=alpha_f32[:], in_=alpha_raw[:])
+        nc.gpsimd.tensor_copy(out=alpha_f32[:], in_=alpha_raw[:])
         gain1 = consts.tile([P, PACK], F32)
-        nc.vector.tensor_copy(out=gain1[:], in_=g1_raw[:])
+        nc.gpsimd.tensor_copy(out=gain1[:], in_=g1_raw[:])
         shift1 = consts.tile([P, PACK], F32)
-        nc.vector.tensor_copy(out=shift1[:], in_=b1_raw[:])
+        nc.gpsimd.tensor_copy(out=shift1[:], in_=b1_raw[:])
         gain3 = consts.tile([P, PACK], F32)
-        nc.vector.tensor_scalar(
+        nc.gpsimd.tensor_scalar(
             out=gain3[:], in0=g3_raw[:], scalar1=alpha_f32[:, 0:1], scalar2=None, op0=ALU.mult
         )
         shift3 = consts.tile([P, PACK], F32)
-        nc.vector.tensor_scalar(
+        nc.gpsimd.tensor_scalar(
             out=shift3[:], in0=b3_raw[:], scalar1=alpha_f32[:, 0:1], scalar2=1.0, op0=ALU.mult, op1=ALU.add
         )
         gains = [gain1, gain3]
@@ -196,14 +207,10 @@ def tile_polymlp_skiplora_pa_t_kernel(
         live = {}
 
         def first_matmuls(g):
-            y1 = pre_pool.tile([P, GROUP, PACK, P], F32)
-            y3 = pre_pool.tile([P, GROUP, PACK, P], F32)
-            pre_norm = [y1, y3]
-            sums = small.tile([P, 2, GROUP], F32)
             by_feature_tile = []
             for j in range(GROUP):
                 cols = slice(P * (GROUP * g + j), P * (GROUP * g + j + 1))
-                acc1 = psum_first.tile([P, D], F32, tag="first")
+                acc1 = psum_turn.tile([P, D], F32, tag="turn")
                 nc.tensor.matmul_mx(
                     out=acc1[:],
                     lhsT=xq_codes[:, cols].bitcast(FP8X4),
@@ -213,7 +220,7 @@ def tile_polymlp_skiplora_pa_t_kernel(
                     start=True,
                     stop=True,
                 )
-                acc3 = psum_first.tile([P, D], F32, tag="first")
+                acc3 = psum_turn.tile([P, D], F32, tag="turn")
                 nc.tensor.matmul(
                     out=acc3[:],
                     lhsT=z2T[:, cols],
@@ -227,11 +234,18 @@ def tile_polymlp_skiplora_pa_t_kernel(
                         acc3[:].rearrange("p (t m) -> p t m", t=PACK),
                     ]
                 )
+            live[g] = {"by_feature_tile": by_feature_tile}
+
+        def add_first_biases(g):
+            y1 = pre_pool.tile([P, GROUP, PACK, P], F32)
+            y3 = pre_pool.tile([P, GROUP, PACK, P], F32)
+            pre_norm = [y1, y3]
+            sums = small.tile([P, 2, GROUP], F32)
             for j in range(GROUP):
                 for branch in range(2):
                     nc.vector.scalar_tensor_tensor(
                         out=pre_norm[branch][:, j, :, :],
-                        in0=by_feature_tile[j][branch],
+                        in0=live[g]["by_feature_tile"][j][branch],
                         scalar=1.0,
                         in1=biases[branch][:],
                         op0=ALU.mult,
@@ -242,7 +256,8 @@ def tile_polymlp_skiplora_pa_t_kernel(
             nc.vector.tensor_scalar(
                 out=neg_mean[:], in0=sums[:], scalar1=-1.0 / D, scalar2=None, op0=ALU.mult
             )
-            live[g] = {"pre_norm": pre_norm, "neg_mean": neg_mean}
+            live[g]["pre_norm"] = pre_norm
+            live[g]["neg_mean"] = neg_mean
 
         def deviations(g):
             square_sums = small.tile([P, 2, GROUP], F32)
@@ -261,11 +276,12 @@ def tile_polymlp_skiplora_pa_t_kernel(
             nc.scalar.activation(
                 out=std[:], in_=square_sums[:], func=ACT.Sqrt, bias=eps[:, 0:1], scale=1.0 / D
             )
-            live[g]["std"] = std
+            rstd = small.tile([P, 2, GROUP], F32)
+            nc.vector.reciprocal(out=rstd[:], in_=std[:])
+            live[g]["rstd"] = rstd
 
         def normalise(g):
-            rstd = small.tile([P, 2, GROUP], F32)
-            nc.vector.reciprocal(out=rstd[:], in_=live[g]["std"][:])
+            rstd = live[g]["rstd"]
             n1 = stage.tile([P, GROUP, PACK, P], F32)
             n3 = stage.tile([P, GROUP, PACK, P], F32)
             normed = [n1, n3]
@@ -287,7 +303,7 @@ def tile_polymlp_skiplora_pa_t_kernel(
             scaled = [o1T, o3T]
             for branch in range(2):
                 for pair in range(PACK // 2):
-                    nT_bank = psum_tr.tile([P, 2, GROUP * P], F32, tag="tr")
+                    nT_bank = psum_turn.tile([P, 2, GROUP * P], F32, tag="turn")
                     for s in range(2):
                         for j in range(GROUP):
                             nc.tensor.transpose(
@@ -306,7 +322,7 @@ def tile_polymlp_skiplora_pa_t_kernel(
                         )
             live[g]["scaled"] = scaled
 
-        def gate_and_quantise(g):
+        def gate(g):
             o1T, o3T = live[g]["scaled"]
             h_grouped = stage.tile([P, GROUP * P, PACK], BF16, align_bytes=64)
             nc.vector.tensor_tensor(
@@ -315,6 +331,10 @@ def tile_polymlp_skiplora_pa_t_kernel(
                 in1=o3T[:].rearrange("p t (c i) -> p c t i", i=4),
                 op=ALU.mult,
             )
+            live[g]["h_grouped"] = h_grouped
+
+        def last_matmul(g):
+            h_grouped = live[g]["h_grouped"]
             hq_codes = stage.tile([P, GROUP * P], U32, align_bytes=64)
             hq_plane = stage.tile([P, GROUP * P], U8, align_bytes=64)
             nc.vector.quantize_mx(
@@ -322,11 +342,6 @@ def tile_polymlp_skiplora_pa_t_kernel(
                 scales=hq_plane[:],
                 in_=h_grouped[:].rearrange("p w t -> p (w t)"),
             )
-            live[g]["hq"] = (hq_codes, hq_plane)
-
-        def last_matmul(g):
-            hq_codes, hq_plane = live[g]["hq"]
-            result = results.tile([P, GROUP, D], F32)
             banks = []
             for j in range(GROUP):
                 acc_out = psum_last.tile([P, D], F32, tag="last")
@@ -340,20 +355,42 @@ def tile_polymlp_skiplora_pa_t_kernel(
                     stop=True,
                 )
                 banks.append(acc_out)
+            live[g]["banks"] = banks
+
+        def add_bias_and_store(g):
+            result = results.tile([P, GROUP, D], F32)
             for j in range(GROUP):
-                nc.vector.tensor_tensor(out=result[:, j, :], in0=banks[j][:], in1=bias_out[:], op=ALU.add)
+                nc.vector.tensor_tensor(
+                    out=result[:, j, :], in0=live[g]["banks"][j][:], in1=bias_out[:], op=ALU.add
+                )
             nc.sync.dma_start(out=out_view[:, GROUP * g : GROUP * (g + 1), :], in_=result[:])
 
-        groups = TILES // GROUP
-        for k in range(groups + 3):
-            if 0 <= k - 3 < groups:
-                gate_and_quantise(k - 3)
-            if k < groups:
-                first_matmuls(k)
-            if 0 <= k - 3 < groups:
-                last_matmul(k - 3)
-            if 0 <= k - 1 < groups:
+        def in_range(g):
+            return 0 <= g < GROUPS
+
+        def chunks_of_round(k):
+            return [c for c in (2 * k - 1, 2 * k) if 1 <= c < CHUNKS]
+
+        quantise_x(0)
+        first_matmuls(0)
+        for k in range(GROUPS + 5):
+            for c in chunks_of_round(k):
+                quantise_x(c)
+            if in_range(k - 4):
+                gate(k - 4)
+            if in_range(k):
+                add_first_biases(k)
+            if in_range(k - 5):
+                add_bias_and_store(k - 5)
+            if in_range(k - 1):
                 deviations(k - 1)
-                normalise(k - 1)
-            if 0 <= k - 2 < groups:
-                to_features(k - 2)
+            if in_range(k - 2):
+                normalise(k - 2)
+            if in_range(k - 3):
+                to_features(k - 3)
+            if in_range(k + 1):
+                first_matmuls(k + 1)
+            if in_range(k - 4):
+                last_matmul(k - 4)
+            for c in chunks_of_round(k + 1):
+                unpack(c)

@@ -77,7 +77,6 @@ def tile_polymlp_skiplora_pa_t_kernel(
         results = ctx.enter_context(tc.tile_pool(name="results", bufs=3))
         psum_last = ctx.enter_context(tc.psum_pool(name="psum_last", bufs=GROUP))
         psum_turn = ctx.enter_context(tc.psum_pool(name="psum_turn", bufs=8 - GROUP))
-        ctx.enter_context(tc.manual_schedule())
 
         eps = consts.tile([P, 1], F32)
         nc.vector.memset(eps[:], EPS)

@@ -312,19 +312,29 @@ def tile_polymlp_skiplora_pa_t_kernel(
                             )
                     for s in range(2):
                         t = 2 * pair + s
-                        nc.scalar.activation(
-                            out=scaled[branch][:, t, :],
-                            in_=nT_bank[:, s, :],
-                            func=ACT.Identity,
-                            bias=shifts[branch][:, t : t + 1],
-                            scale=gains[branch][:, t : t + 1],
-                        )
+                        if (branch, pair) == (1, 1):
+                            nc.vector.tensor_scalar(
+                                out=scaled[branch][:, t, :],
+                                in0=nT_bank[:, s, :],
+                                scalar1=gains[branch][:, t : t + 1],
+                                scalar2=shifts[branch][:, t : t + 1],
+                                op0=ALU.mult,
+                                op1=ALU.add,
+                            )
+                        else:
+                            nc.scalar.activation(
+                                out=scaled[branch][:, t, :],
+                                in_=nT_bank[:, s, :],
+                                func=ACT.Identity,
+                                bias=shifts[branch][:, t : t + 1],
+                                scale=gains[branch][:, t : t + 1],
+                            )
             live[g]["scaled"] = scaled
 
         def gate(g):
             o1T, o3T = live[g]["scaled"]
             h_grouped = stage.tile([P, GROUP * P, PACK], BF16, align_bytes=64)
-            nc.vector.tensor_tensor(
+            nc.gpsimd.tensor_tensor(
                 out=h_grouped[:].rearrange("p (c i) t -> p c t i", i=4),
                 in0=o1T[:].rearrange("p t (c i) -> p c t i", i=4),
                 in1=o3T[:].rearrange("p t (c i) -> p c t i", i=4),

@@ -72,11 +72,13 @@ def tile_polymlp_skiplora_pa_t_kernel(
         keep = ctx.enter_context(tc.tile_pool(name="keep", bufs=1))
         x_in = ctx.enter_context(tc.tile_pool(name="x_in", bufs=CHUNKS))
         stage = ctx.enter_context(tc.tile_pool(name="stage", bufs=2))
+        x_stage = ctx.enter_context(tc.tile_pool(name="x_stage", bufs=4))
         pre_pool = ctx.enter_context(tc.tile_pool(name="pre_pool", bufs=4))
         small = ctx.enter_context(tc.tile_pool(name="small", bufs=5))
         results = ctx.enter_context(tc.tile_pool(name="results", bufs=3))
         psum_last = ctx.enter_context(tc.psum_pool(name="psum_last", bufs=GROUP))
         psum_turn = ctx.enter_context(tc.psum_pool(name="psum_turn", bufs=8 - GROUP))
+        ctx.enter_context(tc.manual_schedule())
 
         eps = consts.tile([P, 1], F32)
         nc.vector.memset(eps[:], EPS)
@@ -135,7 +137,7 @@ def tile_polymlp_skiplora_pa_t_kernel(
         def unpack(c):
             x_words = x_chunks[c][:].rearrange("p i d -> p (i d)").bitcast(F32)
             words_per_tile = D // 2
-            x_grouped = stage.tile([P, X_CHUNK * P, PACK], BF16, align_bytes=64)
+            x_grouped = x_stage.tile([P, X_CHUNK * P, PACK], BF16, align_bytes=64)
             grouped_words = x_grouped[:].rearrange("p w t -> p (w t)").bitcast(F32)
             for half in range(X_CHUNK // 2):
                 xT_bank = psum_turn.tile([P, 2, 2, P], F32, tag="turn")
@@ -184,6 +186,7 @@ def tile_polymlp_skiplora_pa_t_kernel(
                 nc.vector.tensor_copy(out=spread[:], in_=bias_bank[:])
 
         unpack(0)
+        unpack(1)
 
         alpha_f32 = consts.tile([P, 1], F32)
         nc.gpsimd.tensor_copy(out=alpha_f32[:], in_=alpha_raw[:])
@@ -312,29 +315,19 @@ def tile_polymlp_skiplora_pa_t_kernel(
                             )
                     for s in range(2):
                         t = 2 * pair + s
-                        if (branch, pair) == (1, 1):
-                            nc.vector.tensor_scalar(
-                                out=scaled[branch][:, t, :],
-                                in0=nT_bank[:, s, :],
-                                scalar1=gains[branch][:, t : t + 1],
-                                scalar2=shifts[branch][:, t : t + 1],
-                                op0=ALU.mult,
-                                op1=ALU.add,
-                            )
-                        else:
-                            nc.scalar.activation(
-                                out=scaled[branch][:, t, :],
-                                in_=nT_bank[:, s, :],
-                                func=ACT.Identity,
-                                bias=shifts[branch][:, t : t + 1],
-                                scale=gains[branch][:, t : t + 1],
-                            )
+                        nc.scalar.activation(
+                            out=scaled[branch][:, t, :],
+                            in_=nT_bank[:, s, :],
+                            func=ACT.Identity,
+                            bias=shifts[branch][:, t : t + 1],
+                            scale=gains[branch][:, t : t + 1],
+                        )
             live[g]["scaled"] = scaled
 
         def gate(g):
             o1T, o3T = live[g]["scaled"]
             h_grouped = stage.tile([P, GROUP * P, PACK], BF16, align_bytes=64)
-            nc.gpsimd.tensor_tensor(
+            nc.vector.tensor_tensor(
                 out=h_grouped[:].rearrange("p (c i) t -> p c t i", i=4),
                 in0=o1T[:].rearrange("p t (c i) -> p c t i", i=4),
                 in1=o3T[:].rearrange("p t (c i) -> p c t i", i=4),
@@ -378,13 +371,12 @@ def tile_polymlp_skiplora_pa_t_kernel(
             return 0 <= g < GROUPS
 
         def chunks_of_round(k):
-            return [c for c in (2 * k - 1, 2 * k) if 1 <= c < CHUNKS]
+            return [c for c in (2 * k + 2, 2 * k + 3) if 2 <= c < CHUNKS]
 
         quantise_x(0)
+        quantise_x(1)
         first_matmuls(0)
         for k in range(GROUPS + 5):
-            for c in chunks_of_round(k):
-                quantise_x(c)
             if in_range(k - 4):
                 gate(k - 4)
             if in_range(k):
@@ -397,9 +389,11 @@ def tile_polymlp_skiplora_pa_t_kernel(
                 normalise(k - 2)
             if in_range(k - 3):
                 to_features(k - 3)
+            for c in chunks_of_round(k):
+                unpack(c)
             if in_range(k + 1):
                 first_matmuls(k + 1)
             if in_range(k - 4):
                 last_matmul(k - 4)
-            for c in chunks_of_round(k + 1):
-                unpack(c)
+            for c in chunks_of_round(k - 1):
+                quantise_x(c)

@@ -83,7 +83,7 @@ def tile_polymlp_skiplora_pa_t_kernel(
         eps = consts.tile([P, 1], F32)
         nc.vector.memset(eps[:], EPS)
         table_warm = consts.tile([P, 1], F32)
-        nc.scalar.activation(out=table_warm[:], in_=eps[:], func=ACT.Sqrt)
+        nc.scalar.activation(out=table_warm[:], in_=eps[:], func=ACT.Abs_reciprocal_sqrt)
 
         ident_f32 = consts.tile([P, P], F32)
         make_identity(nc, ident_f32[:])
@@ -254,12 +254,8 @@ def tile_polymlp_skiplora_pa_t_kernel(
                         op1=ALU.add,
                         accum_out=sums[:, branch, j : j + 1],
                     )
-            neg_mean = small.tile([P, 2, GROUP], F32)
-            nc.vector.tensor_scalar(
-                out=neg_mean[:], in0=sums[:], scalar1=-1.0 / D, scalar2=None, op0=ALU.mult
-            )
             live[g]["pre_norm"] = pre_norm
-            live[g]["neg_mean"] = neg_mean
+            live[g]["sums"] = sums
 
         def deviations(g):
             square_sums = small.tile([P, 2, GROUP], F32)
@@ -270,20 +266,22 @@ def tile_polymlp_skiplora_pa_t_kernel(
                         out=squares[:],
                         in_=live[g]["pre_norm"][branch][:, j, :, :].rearrange("p t m -> p (t m)"),
                         func=ACT.Square,
-                        bias=live[g]["neg_mean"][:, branch, j : j + 1],
-                        scale=1.0,
+                        bias=live[g]["sums"][:, branch, j : j + 1],
+                        scale=-float(D),
                         accum_out=square_sums[:, branch, j : j + 1],
                     )
-            std = small.tile([P, 2, GROUP], F32)
-            nc.scalar.activation(
-                out=std[:], in_=square_sums[:], func=ACT.Sqrt, bias=eps[:, 0:1], scale=1.0 / D
-            )
             rstd = small.tile([P, 2, GROUP], F32)
-            nc.vector.reciprocal(out=rstd[:], in_=std[:])
+            nc.scalar.activation(
+                out=rstd[:], in_=square_sums[:], func=ACT.Abs_reciprocal_sqrt, bias=eps[:, 0:1], scale=1.0 / D**3
+            )
             live[g]["rstd"] = rstd
 
         def normalise(g):
             rstd = live[g]["rstd"]
+            neg_mean = small.tile([P, 2, GROUP], F32)
+            nc.gpsimd.tensor_scalar(
+                out=neg_mean[:], in0=live[g]["sums"][:], scalar1=-1.0 / D, scalar2=0.0, op0=ALU.mult, op1=ALU.add
+            )
             n1 = stage.tile([P, GROUP, PACK, P], F32)
             n3 = stage.tile([P, GROUP, PACK, P], F32)
             normed = [n1, n3]
@@ -292,7 +290,7 @@ def tile_polymlp_skiplora_pa_t_kernel(
                     nc.gpsimd.tensor_scalar(
                         out=normed[branch][:, j, :, :],
                         in0=live[g]["pre_norm"][branch][:, j, :, :],
-                        scalar1=live[g]["neg_mean"][:, branch, j : j + 1],
+                        scalar1=neg_mean[:, branch, j : j + 1],
                         scalar2=rstd[:, branch, j : j + 1],
                         op0=ALU.add,
                         op1=ALU.mult,

@@ -20,9 +20,25 @@ DQ = 128
 EPS = 1e-6
 TILES = TOKENS // P
 GROUP = 2
-X_CHUNK = 4
-CHUNKS = TILES // X_CHUNK
 GROUPS = TILES // GROUP
+PIECES = 2 * GROUP
+CHUNK_TILES = [2, 2] + [4] * 7
+CHUNK_START = [sum(CHUNK_TILES[:c]) for c in range(len(CHUNK_TILES))]
+CHUNKS = len(CHUNK_TILES)
+
+AHEAD_F = 2
+LAG_SQ = 2
+LAG_N = 7
+LAG_T = 10
+LAG_EV = 12
+LAG_GATE = 17
+LAG_L = 19
+LAG_FI = 22
+UNPACK_SLOT = [-6, -5, -4, -3, -2, -1, 0, 1, 2]
+QX_LAG = 2
+X_ON_VECTOR = [0, 0, 1, 1, 1, 1, 1, 1, 1]
+N_FIRST, N_TURN, N_LAST = 3, 3, 2
+PRE_BUFS, OUT_BUFS = 5, 3
 
 FLOPS = 2 * TOKENS * D * D * 2 + 2 * TOKENS * DQ * D
 
@@ -72,12 +88,14 @@ def tile_polymlp_skiplora_pa_t_kernel(
         keep = ctx.enter_context(tc.tile_pool(name="keep", bufs=1))
         x_in = ctx.enter_context(tc.tile_pool(name="x_in", bufs=CHUNKS))
         stage = ctx.enter_context(tc.tile_pool(name="stage", bufs=2))
+        scaled_pool = ctx.enter_context(tc.tile_pool(name="scaled_pool", bufs=OUT_BUFS))
         x_stage = ctx.enter_context(tc.tile_pool(name="x_stage", bufs=4))
-        pre_pool = ctx.enter_context(tc.tile_pool(name="pre_pool", bufs=4))
-        small = ctx.enter_context(tc.tile_pool(name="small", bufs=5))
+        pre_pool = ctx.enter_context(tc.tile_pool(name="pre_pool", bufs=PRE_BUFS))
+        small = ctx.enter_context(tc.tile_pool(name="small", bufs=PRE_BUFS + 2))
         results = ctx.enter_context(tc.tile_pool(name="results", bufs=3))
-        psum_last = ctx.enter_context(tc.psum_pool(name="psum_last", bufs=GROUP))
-        psum_turn = ctx.enter_context(tc.psum_pool(name="psum_turn", bufs=8 - GROUP))
+        psum_first = ctx.enter_context(tc.psum_pool(name="psum_first", bufs=N_FIRST))
+        psum_turn = ctx.enter_context(tc.psum_pool(name="psum_turn", bufs=N_TURN))
+        psum_last = ctx.enter_context(tc.psum_pool(name="psum_last", bufs=N_LAST))
         ctx.enter_context(tc.manual_schedule())
 
         eps = consts.tile([P, 1], F32)
@@ -93,11 +111,12 @@ def tile_polymlp_skiplora_pa_t_kernel(
         x_chunks = []
         z_chunks = []
         for c in range(CHUNKS):
-            x_chunk = x_in.tile([P, X_CHUNK, D], BF16)
-            nc.sync.dma_start(out=x_chunk[:], in_=x_view[:, X_CHUNK * c : X_CHUNK * (c + 1), :])
+            tiles = slice(CHUNK_START[c], CHUNK_START[c] + CHUNK_TILES[c])
+            x_chunk = x_in.tile([P, CHUNK_TILES[c], D], BF16)
+            nc.sync.dma_start(out=x_chunk[:], in_=x_view[:, tiles, :])
             x_chunks.append(x_chunk)
-            z_chunk = x_in.tile([P, X_CHUNK, DQ], BF16)
-            nc.sync.dma_start(out=z_chunk[:], in_=z_view[:, X_CHUNK * c : X_CHUNK * (c + 1), :])
+            z_chunk = x_in.tile([P, CHUNK_TILES[c], DQ], BF16)
+            nc.sync.dma_start(out=z_chunk[:], in_=z_view[:, tiles, :])
             z_chunks.append(z_chunk)
             if c == 0:
                 w1_codes, w1_plane = load_mx_weight(nc, consts, U1_w_words, U1_w_scales, "w1")
@@ -132,14 +151,15 @@ def tile_polymlp_skiplora_pa_t_kernel(
         grouped_x = {}
 
         def chunk_columns(c):
-            return slice(X_CHUNK * P * c, X_CHUNK * P * (c + 1))
+            return slice(P * CHUNK_START[c], P * (CHUNK_START[c] + CHUNK_TILES[c]))
 
         def unpack(c):
+            n_tiles = CHUNK_TILES[c]
             x_words = x_chunks[c][:].rearrange("p i d -> p (i d)").bitcast(F32)
             words_per_tile = D // 2
-            x_grouped = x_stage.tile([P, X_CHUNK * P, PACK], BF16, align_bytes=64)
+            x_grouped = x_stage.tile([P, 4 * P, PACK], BF16, align_bytes=64)
             grouped_words = x_grouped[:].rearrange("p w t -> p (w t)").bitcast(F32)
-            for half in range(X_CHUNK // 2):
+            for half in range(n_tiles // 2):
                 xT_bank = psum_turn.tile([P, 2, 2, P], F32, tag="turn")
                 for i in range(2):
                     first = words_per_tile * (2 * half + i)
@@ -149,15 +169,16 @@ def tile_polymlp_skiplora_pa_t_kernel(
                             x_words[:, first + u : first + words_per_tile : 2],
                             ident_f32[:],
                         )
-                nc.scalar.copy(
+                copy = nc.vector.tensor_copy if half < X_ON_VECTOR[c] else nc.scalar.copy
+                copy(
                     out=grouped_words[:, 4 * P * half : 4 * P * (half + 1)].rearrange(
                         "p (i w u) -> p i w u", i=2, u=2
                     ),
                     in_=xT_bank[:].rearrange("p i u w -> p i w u"),
                 )
             grouped_x[c] = x_grouped
-            zT_bank = psum_last.tile([P, X_CHUNK, P], BF16, tag="last")
-            for i in range(X_CHUNK):
+            zT_bank = psum_last.tile([P, n_tiles, P], BF16, tag="last")
+            for i in range(n_tiles):
                 nc.tensor.transpose(zT_bank[:, i, :], z_chunks[c][:, i, :], ident_bf16[:])
             nc.scalar.copy(out=z2T[:, chunk_columns(c)], in_=zT_bank[:].rearrange("p i w -> p (i w)"))
 
@@ -165,7 +186,7 @@ def tile_polymlp_skiplora_pa_t_kernel(
             nc.vector.quantize_mx(
                 out=xq_codes[:, chunk_columns(c)].bitcast(FP8X4),
                 scales=xq_plane[:, chunk_columns(c)],
-                in_=grouped_x[c][:].rearrange("p w t -> p (w t)"),
+                in_=grouped_x[c][:, 0 : P * CHUNK_TILES[c], :].rearrange("p w t -> p (w t)"),
             )
 
         u3T_bank = psum_last.tile([P, PACK, P], BF16, tag="last")
@@ -178,15 +199,12 @@ def tile_polymlp_skiplora_pa_t_kernel(
         bias3 = consts.tile([P, PACK, P], F32)
         bias_out = consts.tile([P, D], F32)
         for v, spread in enumerate([bias1, bias3, bias_out]):
-            bias_bank = psum_turn.tile([P, D], F32, tag="turn")
+            bias_bank = psum_first.tile([P, D], F32, tag="first")
             nc.tensor.matmul(out=bias_bank[:], lhsT=ones[:], rhs=bias_rows[:, v, :], start=True, stop=True)
             if v < 2:
                 nc.vector.tensor_copy(out=spread[:], in_=bias_bank[:].rearrange("p (m t) -> p t m", t=PACK))
             else:
                 nc.vector.tensor_copy(out=spread[:], in_=bias_bank[:])
-
-        unpack(0)
-        unpack(1)
 
         alpha_f32 = consts.tile([P, 1], F32)
         nc.gpsimd.tensor_copy(out=alpha_f32[:], in_=alpha_raw[:])
@@ -208,13 +226,13 @@ def tile_polymlp_skiplora_pa_t_kernel(
 
         live = {}
 
-        def first_matmuls(g):
-            by_feature_tile = []
-            for j in range(GROUP):
-                cols = slice(P * (GROUP * g + j), P * (GROUP * g + j + 1))
-                acc1 = psum_turn.tile([P, D], F32, tag="turn")
+        def first_matmul(g, piece):
+            j, branch = divmod(piece, 2)
+            cols = slice(P * (GROUP * g + j), P * (GROUP * g + j + 1))
+            acc = psum_first.tile([P, D], F32, tag="first")
+            if branch == 0:
                 nc.tensor.matmul_mx(
-                    out=acc1[:],
+                    out=acc[:],
                     lhsT=xq_codes[:, cols].bitcast(FP8X4),
                     lhsT_scale=xq_plane[:, cols],
                     rhs=w1_codes[:].bitcast(FP8X4),
@@ -222,105 +240,108 @@ def tile_polymlp_skiplora_pa_t_kernel(
                     start=True,
                     stop=True,
                 )
-                acc3 = psum_turn.tile([P, D], F32, tag="turn")
+                by_feature_tile = acc[:].rearrange("p (m t) -> p t m", t=PACK)
+            else:
                 nc.tensor.matmul(
-                    out=acc3[:],
+                    out=acc[:],
                     lhsT=z2T[:, cols],
                     rhs=u3T[:].rearrange("k t m -> k (t m)"),
                     start=True,
                     stop=True,
                 )
-                by_feature_tile.append(
-                    [
-                        acc1[:].rearrange("p (m t) -> p t m", t=PACK),
-                        acc3[:].rearrange("p (t m) -> p t m", t=PACK),
-                    ]
-                )
-            live[g] = {"by_feature_tile": by_feature_tile}
+                by_feature_tile = acc[:].rearrange("p (t m) -> p t m", t=PACK)
+            live.setdefault(g, {})[("first", piece)] = by_feature_tile
 
-        def add_first_biases(g):
-            y1 = pre_pool.tile([P, GROUP, PACK, P], F32)
-            y3 = pre_pool.tile([P, GROUP, PACK, P], F32)
-            pre_norm = [y1, y3]
-            sums = small.tile([P, 2, GROUP], F32)
-            for j in range(GROUP):
-                for branch in range(2):
-                    nc.vector.scalar_tensor_tensor(
-                        out=pre_norm[branch][:, j, :, :],
-                        in0=live[g]["by_feature_tile"][j][branch],
-                        scalar=1.0,
-                        in1=biases[branch][:],
-                        op0=ALU.mult,
-                        op1=ALU.add,
-                        accum_out=sums[:, branch, j : j + 1],
-                    )
-            live[g]["pre_norm"] = pre_norm
-            live[g]["sums"] = sums
+        def add_first_bias(g, piece):
+            j, branch = divmod(piece, 2)
+            if piece == 0:
+                y1 = pre_pool.tile([P, GROUP, PACK, P], F32)
+                y3 = pre_pool.tile([P, GROUP, PACK, P], F32)
+                sums = small.tile([P, 2, GROUP], F32)
+                live[g]["pre_norm"] = [y1, y3]
+                live[g]["sums"] = sums
+            nc.vector.scalar_tensor_tensor(
+                out=live[g]["pre_norm"][branch][:, j, :, :],
+                in0=live[g][("first", piece)],
+                scalar=1.0,
+                in1=biases[branch][:],
+                op0=ALU.mult,
+                op1=ALU.add,
+                accum_out=live[g]["sums"][:, branch, j : j + 1],
+            )
 
-        def deviations(g):
-            square_sums = small.tile([P, 2, GROUP], F32)
-            for branch in range(2):
-                for j in range(GROUP):
-                    squares = stage.tile([P, D], F32)
-                    nc.scalar.activation(
-                        out=squares[:],
-                        in_=live[g]["pre_norm"][branch][:, j, :, :].rearrange("p t m -> p (t m)"),
-                        func=ACT.Square,
-                        bias=live[g]["sums"][:, branch, j : j + 1],
-                        scale=-float(D),
-                        accum_out=square_sums[:, branch, j : j + 1],
-                    )
-            rstd = small.tile([P, 2, GROUP], F32)
+        def square(g, piece):
+            j, branch = divmod(piece, 2)
+            if piece == 0:
+                square_sums = small.tile([P, 2, GROUP], F32)
+                live[g]["square_sums"] = square_sums
+            squares = stage.tile([P, D], F32)
             nc.scalar.activation(
-                out=rstd[:], in_=square_sums[:], func=ACT.Abs_reciprocal_sqrt, bias=eps[:, 0:1], scale=1.0 / D**3
+                out=squares[:],
+                in_=live[g]["pre_norm"][branch][:, j, :, :].rearrange("p t m -> p (t m)"),
+                func=ACT.Square,
+                bias=live[g]["sums"][:, branch, j : j + 1],
+                scale=-float(D),
+                accum_out=live[g]["square_sums"][:, branch, j : j + 1],
             )
-            live[g]["rstd"] = rstd
+            if piece == PIECES - 1:
+                rstd = small.tile([P, 2, GROUP], F32)
+                nc.scalar.activation(
+                    out=rstd[:],
+                    in_=live[g]["square_sums"][:],
+                    func=ACT.Abs_reciprocal_sqrt,
+                    bias=eps[:, 0:1],
+                    scale=1.0 / D**3,
+                )
+                live[g]["rstd"] = rstd
 
-        def normalise(g):
-            rstd = live[g]["rstd"]
-            neg_mean = small.tile([P, 2, GROUP], F32)
+        def normalise(g, piece):
+            branch, j = divmod(piece, 2)
+            if piece == 0:
+                neg_mean = small.tile([P, 2, GROUP], F32)
+                nc.gpsimd.tensor_scalar(
+                    out=neg_mean[:], in0=live[g]["sums"][:], scalar1=-1.0 / D, scalar2=0.0, op0=ALU.mult, op1=ALU.add
+                )
+                n1 = stage.tile([P, GROUP, PACK, P], F32)
+                n3 = stage.tile([P, GROUP, PACK, P], F32)
+                live[g]["normed"] = [n1, n3]
+                live[g]["neg_mean"] = neg_mean
             nc.gpsimd.tensor_scalar(
-                out=neg_mean[:], in0=live[g]["sums"][:], scalar1=-1.0 / D, scalar2=0.0, op0=ALU.mult, op1=ALU.add
+                out=live[g]["normed"][branch][:, j, :, :],
+                in0=live[g]["pre_norm"][branch][:, j, :, :],
+                scalar1=live[g]["neg_mean"][:, branch, j : j + 1],
+                scalar2=live[g]["rstd"][:, branch, j : j + 1],
+                op0=ALU.add,
+                op1=ALU.mult,
             )
-            n1 = stage.tile([P, GROUP, PACK, P], F32)
-            n3 = stage.tile([P, GROUP, PACK, P], F32)
-            normed = [n1, n3]
-            for branch in range(2):
-                for j in range(GROUP):
-                    nc.gpsimd.tensor_scalar(
-                        out=normed[branch][:, j, :, :],
-                        in0=live[g]["pre_norm"][branch][:, j, :, :],
-                        scalar1=neg_mean[:, branch, j : j + 1],
-                        scalar2=rstd[:, branch, j : j + 1],
-                        op0=ALU.add,
-                        op1=ALU.mult,
-                    )
-            live[g]["normed"] = normed
 
-        def to_features(g):
-            o1T = stage.tile([P, PACK, GROUP * P], F32)
-            o3T = stage.tile([P, PACK, GROUP * P], F32)
-            scaled = [o1T, o3T]
-            for branch in range(2):
-                for pair in range(PACK // 2):
-                    nT_bank = psum_turn.tile([P, 2, GROUP * P], F32, tag="turn")
-                    for s in range(2):
-                        for j in range(GROUP):
-                            nc.tensor.transpose(
-                                nT_bank[:, s, P * j : P * (j + 1)],
-                                live[g]["normed"][branch][:, j, 2 * pair + s, :],
-                                ident_f32[:],
-                            )
-                    for s in range(2):
-                        t = 2 * pair + s
-                        nc.scalar.activation(
-                            out=scaled[branch][:, t, :],
-                            in_=nT_bank[:, s, :],
-                            func=ACT.Identity,
-                            bias=shifts[branch][:, t : t + 1],
-                            scale=gains[branch][:, t : t + 1],
-                        )
-            live[g]["scaled"] = scaled
+        def transposes(g, piece):
+            branch, pair = divmod(piece, 2)
+            nT_bank = psum_turn.tile([P, 2, GROUP * P], F32, tag="turn")
+            for s in range(2):
+                for j in range(GROUP):
+                    nc.tensor.transpose(
+                        nT_bank[:, s, P * j : P * (j + 1)],
+                        live[g]["normed"][branch][:, j, 2 * pair + s, :],
+                        ident_f32[:],
+                    )
+            live[g][("turned", piece)] = nT_bank
+
+        def gain_and_shift(g, piece):
+            branch, pair = divmod(piece, 2)
+            if piece == 0:
+                o1T = scaled_pool.tile([P, PACK, GROUP * P], F32)
+                o3T = scaled_pool.tile([P, PACK, GROUP * P], F32)
+                live[g]["scaled"] = [o1T, o3T]
+            for s in range(2):
+                t = 2 * pair + s
+                nc.scalar.activation(
+                    out=live[g]["scaled"][branch][:, t, :],
+                    in_=live[g][("turned", piece)][:, s, :],
+                    func=ACT.Identity,
+                    bias=shifts[branch][:, t : t + 1],
+                    scale=gains[branch][:, t : t + 1],
+                )
 
         def gate(g):
             o1T, o3T = live[g]["scaled"]
@@ -333,65 +354,77 @@ def tile_polymlp_skiplora_pa_t_kernel(
             )
             live[g]["h_grouped"] = h_grouped
 
-        def last_matmul(g):
-            h_grouped = live[g]["h_grouped"]
+        def quantise_h(g):
             hq_codes = stage.tile([P, GROUP * P], U32, align_bytes=64)
             hq_plane = stage.tile([P, GROUP * P], U8, align_bytes=64)
             nc.vector.quantize_mx(
                 out=hq_codes[:].bitcast(FP8X4),
                 scales=hq_plane[:],
-                in_=h_grouped[:].rearrange("p w t -> p (w t)"),
+                in_=live[g]["h_grouped"][:].rearrange("p w t -> p (w t)"),
             )
-            banks = []
-            for j in range(GROUP):
-                acc_out = psum_last.tile([P, D], F32, tag="last")
-                nc.tensor.matmul_mx(
-                    out=acc_out[:],
-                    lhsT=hq_codes[:, P * j : P * (j + 1)].bitcast(FP8X4),
-                    lhsT_scale=hq_plane[:, P * j : P * (j + 1)],
-                    rhs=c_codes[:].bitcast(FP8X4),
-                    rhs_scale=c_plane[:],
-                    start=True,
-                    stop=True,
-                )
-                banks.append(acc_out)
-            live[g]["banks"] = banks
+            live[g]["hq"] = (hq_codes, hq_plane)
 
-        def add_bias_and_store(g):
-            result = results.tile([P, GROUP, D], F32)
-            for j in range(GROUP):
-                nc.vector.tensor_tensor(
-                    out=result[:, j, :], in0=live[g]["banks"][j][:], in1=bias_out[:], op=ALU.add
-                )
-            nc.sync.dma_start(out=out_view[:, GROUP * g : GROUP * (g + 1), :], in_=result[:])
+        def last_matmul(g, j):
+            hq_codes, hq_plane = live[g]["hq"]
+            acc_out = psum_last.tile([P, D], F32, tag="last")
+            nc.tensor.matmul_mx(
+                out=acc_out[:],
+                lhsT=hq_codes[:, P * j : P * (j + 1)].bitcast(FP8X4),
+                lhsT_scale=hq_plane[:, P * j : P * (j + 1)],
+                rhs=c_codes[:].bitcast(FP8X4),
+                rhs_scale=c_plane[:],
+                start=True,
+                stop=True,
+            )
+            live[g][("last", j)] = acc_out
 
-        def in_range(g):
-            return 0 <= g < GROUPS
+        def add_last_bias(g, j):
+            if j == 0:
+                result = results.tile([P, GROUP, D], F32)
+                live[g]["result"] = result
+            result = live[g]["result"]
+            nc.vector.tensor_tensor(out=result[:, j, :], in0=live[g][("last", j)][:], in1=bias_out[:], op=ALU.add)
+            if j == GROUP - 1:
+                nc.sync.dma_start(out=out_view[:, GROUP * g : GROUP * (g + 1), :], in_=result[:])
 
-        def chunks_of_round(k):
-            return [c for c in (2 * k + 2, 2 * k + 3) if 2 <= c < CHUNKS]
+        def piece_at(slot):
+            g, piece = divmod(slot, PIECES)
+            return (g, piece) if 0 <= g < GROUPS else None
 
-        quantise_x(0)
-        quantise_x(1)
-        first_matmuls(0)
-        for k in range(GROUPS + 5):
-            if in_range(k - 4):
-                gate(k - 4)
-            if in_range(k):
-                add_first_biases(k)
-            if in_range(k - 5):
-                add_bias_and_store(k - 5)
-            if in_range(k - 1):
-                deviations(k - 1)
-            if in_range(k - 2):
-                normalise(k - 2)
-            if in_range(k - 3):
-                to_features(k - 3)
-            for c in chunks_of_round(k):
-                unpack(c)
-            if in_range(k + 1):
-                first_matmuls(k + 1)
-            if in_range(k - 4):
-                last_matmul(k - 4)
-            for c in chunks_of_round(k - 1):
-                quantise_x(c)
+        first_slot = min(UNPACK_SLOT)
+        for slot in range(first_slot, PIECES * GROUPS + LAG_FI + GROUP):
+            at = piece_at(slot - LAG_GATE)
+            if at and at[1] == 0:
+                gate(at[0])
+            if at and at[1] == 1:
+                quantise_h(at[0])
+            at = piece_at(slot - LAG_FI)
+            if at and at[1] < GROUP:
+                add_last_bias(at[0], at[1])
+            for c in range(CHUNKS):
+                if UNPACK_SLOT[c] + QX_LAG == slot:
+                    quantise_x(c)
+            at = piece_at(slot)
+            if at:
+                add_first_bias(*at)
+            at = piece_at(slot - LAG_SQ)
+            if at:
+                square(*at)
+            at = piece_at(slot - LAG_EV)
+            if at:
+                gain_and_shift(*at)
+            at = piece_at(slot - LAG_N)
+            if at:
+                normalise(*at)
+            at = piece_at(slot - LAG_T)
+            if at:
+                transposes(*at)
+            at = piece_at(slot + AHEAD_F)
+            if at:
+                first_matmul(*at)
+            at = piece_at(slot - LAG_L)
+            if at and at[1] < GROUP:
+                last_matmul(at[0], at[1])
+            for c in range(CHUNKS):
+                if UNPACK_SLOT[c] == slot:
+                    unpack(c)

@@ -28,17 +28,21 @@ CHUNKS = len(CHUNK_TILES)
 
 AHEAD_F = 2
 LAG_SQ = 2
-LAG_N = 7
-LAG_T = 10
-LAG_EV = 12
-LAG_GATE = 17
-LAG_L = 19
-LAG_FI = 22
+LAG_N = 6
+LAG_T = 8
+LAG_EV = 9
+LAG_GATE = 12
+LAG_L = 15
+LAG_FI = 19
 UNPACK_SLOT = [-6, -5, -4, -3, -2, -1, 0, 1, 2]
 QX_LAG = 2
-X_ON_VECTOR = [0, 0, 1, 1, 1, 1, 1, 1, 1]
+X_ON_VECTOR = [0, 0, 0, 0, 0, 0, 0, 0, 0]
 N_FIRST, N_TURN, N_LAST = 3, 3, 2
+OWN = False
+SCALAR_FROM = 3
 PRE_BUFS, OUT_BUFS = 5, 3
+CONST_A_SLOT, CONST_B_SLOT = -6, 0
+SCALAR_PIECE = 3
 
 FLOPS = 2 * TOKENS * D * D * 2 + 2 * TOKENS * DQ * D
 
@@ -94,6 +98,7 @@ def tile_polymlp_skiplora_pa_t_kernel(
         small = ctx.enter_context(tc.tile_pool(name="small", bufs=PRE_BUFS + 2))
         results = ctx.enter_context(tc.tile_pool(name="results", bufs=3))
         psum_first = ctx.enter_context(tc.psum_pool(name="psum_first", bufs=N_FIRST))
+        psum_own = ctx.enter_context(tc.psum_pool(name="psum_own", bufs=1)) if OWN else None
         psum_turn = ctx.enter_context(tc.psum_pool(name="psum_turn", bufs=N_TURN))
         psum_last = ctx.enter_context(tc.psum_pool(name="psum_last", bufs=N_LAST))
         ctx.enter_context(tc.manual_schedule())
@@ -125,12 +130,9 @@ def tile_polymlp_skiplora_pa_t_kernel(
         u3_rows = consts.tile([P, PACK, DQ], BF16)
         nc.scalar.dma_start(out=u3_rows[:], in_=U3_w.rearrange("(m t) k -> m t k", t=PACK))
 
-        bias_rows = consts.tile([P, 3, D], BF16)
-        nc.vector.memset(bias_rows[:], 0.0)
-        for v, vec in enumerate([U1_b, U3_b, C_b]):
-            nc.scalar.dma_start(out=bias_rows[0:1, v, :], in_=vec.unsqueeze(0))
-        ones = consts.tile([P, P], BF16)
-        nc.vector.memset(ones[:], 1.0)
+        first_row = consts.tile([P, P], BF16)
+        nc.vector.memset(first_row[:], 0.0)
+        nc.vector.memset(first_row[0:1, :], 1.0)
 
         def load_by_feature(vec, name):
             column = consts.tile([P, PACK], BF16, name=name)
@@ -138,6 +140,9 @@ def tile_polymlp_skiplora_pa_t_kernel(
             return column
 
         with nc.allow_non_contiguous_dma(reason="four neighbouring elements of a 512-vector to a partition"):
+            u1b_raw = load_by_feature(U1_b, "u1b_raw")
+            u3b_raw = load_by_feature(U3_b, "u3b_raw")
+            cb_raw = load_by_feature(C_b, "cb_raw")
             g1_raw = load_by_feature(ln1_g, "g1_raw")
             b1_raw = load_by_feature(ln1_b, "b1_raw")
             g3_raw = load_by_feature(ln3_g, "g3_raw")
@@ -189,47 +194,94 @@ def tile_polymlp_skiplora_pa_t_kernel(
                 in_=grouped_x[c][:, 0 : P * CHUNK_TILES[c], :].rearrange("p w t -> p (w t)"),
             )
 
-        u3T_bank = psum_last.tile([P, PACK, P], BF16, tag="last")
-        for t in range(PACK):
-            nc.tensor.transpose(u3T_bank[:, t, :], u3_rows[:, t, :], ident_bf16[:])
-        u3T = consts.tile([P, PACK, P], BF16)
-        nc.vector.tensor_copy(out=u3T[:], in_=u3T_bank[:])
+        const = {}
 
+        def as_f32(raw, name):
+            column = consts.tile([P, PACK], F32, name=name)
+            nc.gpsimd.tensor_copy(out=column[:], in_=raw[:])
+            return column
+
+        def spread(column):
+            bank = psum_turn.tile([P, PACK, P], F32, tag="turn")
+            for t in range(PACK):
+                nc.tensor.transpose(bank[:, t, :], column[:, t : t + 1].to_broadcast([P, P]), ident_f32[:])
+            return bank
+
+        u3T = consts.tile([P, PACK, P], BF16)
         bias1 = consts.tile([P, PACK, P], F32)
         bias3 = consts.tile([P, PACK, P], F32)
+        bias3_rows = consts.tile([P, PACK, P], BF16)
         bias_out = consts.tile([P, D], F32)
-        for v, spread in enumerate([bias1, bias3, bias_out]):
-            bias_bank = psum_first.tile([P, D], F32, tag="first")
-            nc.tensor.matmul(out=bias_bank[:], lhsT=ones[:], rhs=bias_rows[:, v, :], start=True, stop=True)
-            if v < 2:
-                nc.vector.tensor_copy(out=spread[:], in_=bias_bank[:].rearrange("p (m t) -> p t m", t=PACK))
-            else:
-                nc.vector.tensor_copy(out=spread[:], in_=bias_bank[:])
-
-        alpha_f32 = consts.tile([P, 1], F32)
-        nc.gpsimd.tensor_copy(out=alpha_f32[:], in_=alpha_raw[:])
-        gain1 = consts.tile([P, PACK], F32)
-        nc.gpsimd.tensor_copy(out=gain1[:], in_=g1_raw[:])
-        shift1 = consts.tile([P, PACK], F32)
-        nc.gpsimd.tensor_copy(out=shift1[:], in_=b1_raw[:])
-        gain3 = consts.tile([P, PACK], F32)
-        nc.gpsimd.tensor_scalar(
-            out=gain3[:], in0=g3_raw[:], scalar1=alpha_f32[:, 0:1], scalar2=None, op0=ALU.mult
-        )
-        shift3 = consts.tile([P, PACK], F32)
-        nc.gpsimd.tensor_scalar(
-            out=shift3[:], in0=b3_raw[:], scalar1=alpha_f32[:, 0:1], scalar2=1.0, op0=ALU.mult, op1=ALU.add
-        )
-        gains = [gain1, gain3]
-        shifts = [shift1, shift3]
         biases = [bias1, bias3]
+        gate_gain = consts.tile([P, PACK], F32)
+        gate_shift = consts.tile([P, PACK], F32)
+        offset1_spread = consts.tile([P, PACK, P], F32)
+
+        def constants_of_the_first_matmuls():
+            u3T_bank = psum_last.tile([P, PACK, P], BF16, tag="last")
+            for t in range(PACK):
+                nc.tensor.transpose(u3T_bank[:, t, :], u3_rows[:, t, :], ident_bf16[:])
+            nc.vector.tensor_copy(out=u3T[:], in_=u3T_bank[:])
+            nc.vector.tensor_copy(out=bias1[:], in_=spread(as_f32(u1b_raw, "u1b"))[:])
+            bias3_bank = spread(as_f32(u3b_raw, "u3b"))
+            nc.vector.tensor_copy(out=bias3[:], in_=bias3_bank[:])
+            nc.vector.tensor_copy(out=bias3_rows[:], in_=bias3_bank[:])
+
+        def constants_of_the_gate():
+            nc.vector.tensor_copy(
+                out=bias_out[:].rearrange("p (m t) -> p m t", t=PACK),
+                in_=spread(as_f32(cb_raw, "cb"))[:].rearrange("p t m -> p m t"),
+            )
+            alpha_f32 = consts.tile([P, 1], F32)
+            nc.gpsimd.tensor_copy(out=alpha_f32[:], in_=alpha_raw[:])
+            gain1 = as_f32(g1_raw, "gain1")
+            shift1 = as_f32(b1_raw, "shift1")
+            gain3 = consts.tile([P, PACK], F32)
+            nc.gpsimd.tensor_scalar(
+                out=gain3[:], in0=g3_raw[:], scalar1=alpha_f32[:, 0:1], scalar2=None, op0=ALU.mult
+            )
+            shift3 = consts.tile([P, PACK], F32)
+            nc.gpsimd.tensor_scalar(
+                out=shift3[:], in0=b3_raw[:], scalar1=alpha_f32[:, 0:1], scalar2=1.0, op0=ALU.mult, op1=ALU.add
+            )
+
+            def small_tile(name):
+                return consts.tile([P, PACK], F32, name=name)
+
+            def magnitude(column, name):
+                negative = small_tile(name + "_neg")
+                nc.vector.tensor_scalar(out=negative[:], in0=column[:], scalar1=-1.0, scalar2=None, op0=ALU.mult)
+                result = small_tile(name)
+                nc.vector.tensor_tensor(out=result[:], in0=column[:], in1=negative[:], op=ALU.max)
+                return result
+
+            floor1 = small_tile("floor1")
+            nc.vector.tensor_scalar(
+                out=floor1[:], in0=magnitude(shift1, "abs_shift1")[:], scalar1=2.0**-100, scalar2=2.0**-126,
+                op0=ALU.mult, op1=ALU.max,
+            )
+            large_enough = small_tile("large_enough")
+            nc.vector.tensor_tensor(out=large_enough[:], in0=magnitude(gain1, "abs_gain1")[:], in1=floor1[:], op=ALU.is_ge)
+            safe_gain = small_tile("safe_gain")
+            nc.vector.tensor_tensor(out=safe_gain[:], in0=gain1[:], in1=floor1[:], op=ALU.subtract)
+            nc.vector.tensor_tensor(out=safe_gain[:], in0=safe_gain[:], in1=large_enough[:], op=ALU.mult)
+            nc.vector.tensor_tensor(out=safe_gain[:], in0=safe_gain[:], in1=floor1[:], op=ALU.add)
+            offset1 = small_tile("offset1")
+            nc.vector.reciprocal(out=offset1[:], in_=safe_gain[:])
+            nc.vector.tensor_tensor(out=offset1[:], in0=offset1[:], in1=shift1[:], op=ALU.mult)
+            nc.vector.tensor_tensor(out=gate_gain[:], in0=safe_gain[:], in1=gain3[:], op=ALU.mult)
+            nc.vector.tensor_tensor(out=gate_shift[:], in0=safe_gain[:], in1=shift3[:], op=ALU.mult)
+            nc.vector.tensor_copy(out=offset1_spread[:], in_=spread(offset1)[:])
 
         live = {}
 
         def first_matmul(g, piece):
             j, branch = divmod(piece, 2)
             cols = slice(P * (GROUP * g + j), P * (GROUP * g + j + 1))
-            acc = psum_first.tile([P, D], F32, tag="first")
+            if piece == SCALAR_PIECE and g >= SCALAR_FROM and OWN:
+                acc = psum_own.tile([P, D], F32, tag="own")
+            else:
+                acc = psum_first.tile([P, D], F32, tag="first")
             if branch == 0:
                 nc.tensor.matmul_mx(
                     out=acc[:],
@@ -242,11 +294,19 @@ def tile_polymlp_skiplora_pa_t_kernel(
                 )
                 by_feature_tile = acc[:].rearrange("p (m t) -> p t m", t=PACK)
             else:
+                if piece == SCALAR_PIECE and g >= SCALAR_FROM:
+                    nc.tensor.matmul(
+                        out=acc[:],
+                        lhsT=first_row[:],
+                        rhs=bias3_rows[:].rearrange("k t m -> k (t m)"),
+                        start=True,
+                        stop=False,
+                    )
                 nc.tensor.matmul(
                     out=acc[:],
                     lhsT=z2T[:, cols],
                     rhs=u3T[:].rearrange("k t m -> k (t m)"),
-                    start=True,
+                    start=not (piece == SCALAR_PIECE and g >= SCALAR_FROM),
                     stop=True,
                 )
                 by_feature_tile = acc[:].rearrange("p (t m) -> p t m", t=PACK)
@@ -260,6 +320,14 @@ def tile_polymlp_skiplora_pa_t_kernel(
                 sums = small.tile([P, 2, GROUP], F32)
                 live[g]["pre_norm"] = [y1, y3]
                 live[g]["sums"] = sums
+            if piece == SCALAR_PIECE and g >= SCALAR_FROM:
+                nc.scalar.activation(
+                    out=live[g]["pre_norm"][branch][:, j, :, :],
+                    in_=live[g][("first", piece)],
+                    func=ACT.Identity,
+                    accum_out=live[g]["sums"][:, branch, j : j + 1],
+                )
+                return
             nc.vector.scalar_tensor_tensor(
                 out=live[g]["pre_norm"][branch][:, j, :, :],
                 in0=live[g][("first", piece)],
@@ -296,7 +364,7 @@ def tile_polymlp_skiplora_pa_t_kernel(
                 live[g]["rstd"] = rstd
 
         def normalise(g, piece):
-            branch, j = divmod(piece, 2)
+            branch, j = 1 - piece // 2, piece % 2
             if piece == 0:
                 neg_mean = small.tile([P, 2, GROUP], F32)
                 nc.gpsimd.tensor_scalar(
@@ -316,43 +384,54 @@ def tile_polymlp_skiplora_pa_t_kernel(
             )
 
         def transposes(g, piece):
-            branch, pair = divmod(piece, 2)
-            nT_bank = psum_turn.tile([P, 2, GROUP * P], F32, tag="turn")
-            for s in range(2):
-                for j in range(GROUP):
-                    nc.tensor.transpose(
-                        nT_bank[:, s, P * j : P * (j + 1)],
-                        live[g]["normed"][branch][:, j, 2 * pair + s, :],
-                        ident_f32[:],
+            if piece < 2:
+                pair = piece
+                nT_bank = psum_turn.tile([P, 2, GROUP * P], F32, tag="turn")
+                for s in range(2):
+                    for j in range(GROUP):
+                        nc.tensor.transpose(
+                            nT_bank[:, s, P * j : P * (j + 1)],
+                            live[g]["normed"][1][:, j, 2 * pair + s, :],
+                            ident_f32[:],
+                        )
+            else:
+                j = piece - 2
+                nT_bank = psum_turn.tile([P, PACK, P], F32, tag="turn")
+                for t in range(PACK):
+                    nc.tensor.matmul(
+                        out=nT_bank[:, t, :], lhsT=offset1_spread[:, t, :], rhs=ident_f32[:],
+                        is_transpose=True, start=True, stop=False,
+                    )
+                    nc.tensor.matmul(
+                        out=nT_bank[:, t, :], lhsT=live[g]["normed"][0][:, j, t, :], rhs=ident_f32[:],
+                        is_transpose=True, start=False, stop=True,
                     )
             live[g][("turned", piece)] = nT_bank
 
-        def gain_and_shift(g, piece):
-            branch, pair = divmod(piece, 2)
-            if piece == 0:
-                o1T = scaled_pool.tile([P, PACK, GROUP * P], F32)
+        def gain_and_shift(g, pair):
+            if pair == 0:
                 o3T = scaled_pool.tile([P, PACK, GROUP * P], F32)
-                live[g]["scaled"] = [o1T, o3T]
+                live[g]["scaled"] = o3T
             for s in range(2):
                 t = 2 * pair + s
                 nc.scalar.activation(
-                    out=live[g]["scaled"][branch][:, t, :],
-                    in_=live[g][("turned", piece)][:, s, :],
+                    out=live[g]["scaled"][:, t, :],
+                    in_=live[g][("turned", pair)][:, s, :],
                     func=ACT.Identity,
-                    bias=shifts[branch][:, t : t + 1],
-                    scale=gains[branch][:, t : t + 1],
+                    bias=gate_shift[:, t : t + 1],
+                    scale=gate_gain[:, t : t + 1],
                 )
 
-        def gate(g):
-            o1T, o3T = live[g]["scaled"]
-            h_grouped = stage.tile([P, GROUP * P, PACK], BF16, align_bytes=64)
+        def gate(g, j):
+            if j == 0:
+                h_grouped = stage.tile([P, GROUP * P, PACK], BF16, align_bytes=64)
+                live[g]["h_grouped"] = h_grouped
             nc.vector.tensor_tensor(
-                out=h_grouped[:].rearrange("p (c i) t -> p c t i", i=4),
-                in0=o1T[:].rearrange("p t (c i) -> p c t i", i=4),
-                in1=o3T[:].rearrange("p t (c i) -> p c t i", i=4),
+                out=live[g]["h_grouped"][:, P * j : P * (j + 1), :].rearrange("p (c i) t -> p c t i", i=4),
+                in0=live[g][("turned", 2 + j)][:].rearrange("p t (c i) -> p c t i", i=4),
+                in1=live[g]["scaled"][:, :, P * j : P * (j + 1)].rearrange("p t (c i) -> p c t i", i=4),
                 op=ALU.mult,
             )
-            live[g]["h_grouped"] = h_grouped
 
         def quantise_h(g):
             hq_codes = stage.tile([P, GROUP * P], U32, align_bytes=64)
@@ -392,26 +471,28 @@ def tile_polymlp_skiplora_pa_t_kernel(
             return (g, piece) if 0 <= g < GROUPS else None
 
         first_slot = min(UNPACK_SLOT)
-        for slot in range(first_slot, PIECES * GROUPS + LAG_FI + GROUP):
+        for slot in range(first_slot, PIECES * GROUPS + LAG_FI + 1):
             at = piece_at(slot - LAG_GATE)
-            if at and at[1] == 0:
-                gate(at[0])
-            if at and at[1] == 1:
-                quantise_h(at[0])
-            at = piece_at(slot - LAG_FI)
             if at and at[1] < GROUP:
-                add_last_bias(at[0], at[1])
+                gate(at[0], at[1])
+            at = piece_at(slot - LAG_FI)
+            if at and at[1] == 0:
+                for j in range(GROUP):
+                    add_last_bias(at[0], j)
             for c in range(CHUNKS):
                 if UNPACK_SLOT[c] + QX_LAG == slot:
                     quantise_x(c)
             at = piece_at(slot)
             if at:
                 add_first_bias(*at)
+            at = piece_at(slot - LAG_GATE)
+            if at and at[1] == GROUP:
+                quantise_h(at[0])
             at = piece_at(slot - LAG_SQ)
             if at:
                 square(*at)
             at = piece_at(slot - LAG_EV)
-            if at:
+            if at and at[1] < 2:
                 gain_and_shift(*at)
             at = piece_at(slot - LAG_N)
             if at:
@@ -428,3 +509,7 @@ def tile_polymlp_skiplora_pa_t_kernel(
             for c in range(CHUNKS):
                 if UNPACK_SLOT[c] == slot:
                     unpack(c)
+            if slot == CONST_A_SLOT:
+                constants_of_the_first_matmuls()
+            if slot == CONST_B_SLOT:
+                constants_of_the_gate()

@@ -35,13 +35,14 @@ LAG_GATE = 12
 LAG_L = 15
 LAG_FI = 19
 UNPACK_SLOT = [-6, -5, -4, -3, -2, -1, 0, 1, 2]
-QX_LAG = 2
+QX_LAG = 4
 X_ON_VECTOR = [0, 0, 0, 0, 0, 0, 0, 0, 0]
 N_FIRST, N_TURN, N_LAST = 3, 3, 2
 OWN = False
 SCALAR_FROM = 3
 PRE_BUFS, OUT_BUFS = 5, 3
-CONST_A_SLOT, CONST_B_SLOT = -6, 0
+CONST_A_SLOT, CONST_B_SLOT, CONST_C_SLOT = -6, -6, 5
+STORE_BY_TILE = 1
 SCALAR_PIECE = 3
 
 FLOPS = 2 * TOKENS * D * D * 2 + 2 * TOKENS * DQ * D
@@ -227,11 +228,16 @@ def tile_polymlp_skiplora_pa_t_kernel(
             nc.vector.tensor_copy(out=bias3[:], in_=bias3_bank[:])
             nc.vector.tensor_copy(out=bias3_rows[:], in_=bias3_bank[:])
 
-        def constants_of_the_gate():
+        offset1 = consts.tile([P, PACK], F32)
+
+        def spreads_of_the_gate():
             nc.vector.tensor_copy(
                 out=bias_out[:].rearrange("p (m t) -> p m t", t=PACK),
                 in_=spread(as_f32(cb_raw, "cb"))[:].rearrange("p t m -> p m t"),
             )
+            nc.vector.tensor_copy(out=offset1_spread[:], in_=spread(offset1)[:])
+
+        def constants_of_the_gate():
             alpha_f32 = consts.tile([P, 1], F32)
             nc.gpsimd.tensor_copy(out=alpha_f32[:], in_=alpha_raw[:])
             gain1 = as_f32(g1_raw, "gain1")
@@ -266,12 +272,10 @@ def tile_polymlp_skiplora_pa_t_kernel(
             nc.vector.tensor_tensor(out=safe_gain[:], in0=gain1[:], in1=floor1[:], op=ALU.subtract)
             nc.vector.tensor_tensor(out=safe_gain[:], in0=safe_gain[:], in1=large_enough[:], op=ALU.mult)
             nc.vector.tensor_tensor(out=safe_gain[:], in0=safe_gain[:], in1=floor1[:], op=ALU.add)
-            offset1 = small_tile("offset1")
             nc.vector.reciprocal(out=offset1[:], in_=safe_gain[:])
             nc.vector.tensor_tensor(out=offset1[:], in0=offset1[:], in1=shift1[:], op=ALU.mult)
             nc.vector.tensor_tensor(out=gate_gain[:], in0=safe_gain[:], in1=gain3[:], op=ALU.mult)
             nc.vector.tensor_tensor(out=gate_shift[:], in0=safe_gain[:], in1=shift3[:], op=ALU.mult)
-            nc.vector.tensor_copy(out=offset1_spread[:], in_=spread(offset1)[:])
 
         live = {}
 
@@ -463,7 +467,9 @@ def tile_polymlp_skiplora_pa_t_kernel(
                 live[g]["result"] = result
             result = live[g]["result"]
             nc.vector.tensor_tensor(out=result[:, j, :], in0=live[g][("last", j)][:], in1=bias_out[:], op=ALU.add)
-            if j == GROUP - 1:
+            if STORE_BY_TILE:
+                nc.sync.dma_start(out=out_view[:, GROUP * g + j, :], in_=result[:, j, :])
+            elif j == GROUP - 1:
                 nc.sync.dma_start(out=out_view[:, GROUP * g : GROUP * (g + 1), :], in_=result[:])
 
         def piece_at(slot):
@@ -513,3 +519,5 @@ def tile_polymlp_skiplora_pa_t_kernel(
                 constants_of_the_first_matmuls()
             if slot == CONST_B_SLOT:
                 constants_of_the_gate()
+            if slot == CONST_C_SLOT:
+                spreads_of_the_gate()

@@ -431,9 +431,9 @@ def tile_polymlp_skiplora_pa_t_kernel(
                 h_grouped = stage.tile([P, GROUP * P, PACK], BF16, align_bytes=64)
                 live[g]["h_grouped"] = h_grouped
             nc.vector.tensor_tensor(
-                out=live[g]["h_grouped"][:, P * j : P * (j + 1), :].rearrange("p (c i) t -> p c t i", i=4),
-                in0=live[g][("turned", 2 + j)][:].rearrange("p t (c i) -> p c t i", i=4),
-                in1=live[g]["scaled"][:, :, P * j : P * (j + 1)].rearrange("p t (c i) -> p c t i", i=4),
+                out=live[g]["h_grouped"][:, P * j : P * (j + 1), :].rearrange("p (c i) t -> p c t i", i=8),
+                in0=live[g][("turned", 2 + j)][:].rearrange("p t (c i) -> p c t i", i=8),
+                in1=live[g]["scaled"][:, :, P * j : P * (j + 1)].rearrange("p t (c i) -> p c t i", i=8),
                 op=ALU.mult,
             )
 

@@ -43,6 +43,7 @@ SCALAR_FROM = 3
 PRE_BUFS, OUT_BUFS = 5, 3
 CONST_A_SLOT, CONST_B_SLOT, CONST_C_SLOT = -6, -6, 5
 STORE_BY_TILE = 1
+TOKEN = 1
 SCALAR_PIECE = 3
 
 FLOPS = 2 * TOKENS * D * D * 2 + 2 * TOKENS * DQ * D
@@ -367,17 +368,26 @@ def tile_polymlp_skiplora_pa_t_kernel(
                 )
                 live[g]["rstd"] = rstd
 
-        def normalise(g, piece):
-            branch, j = 1 - piece // 2, piece % 2
-            if piece == 0:
-                neg_mean = small.tile([P, 2, GROUP], F32)
+        def negative_mean(g):
+            neg_mean = small.tile([P, 2, GROUP], F32)
+            if TOKEN:
+                nc.vector.tensor_scalar(
+                    out=neg_mean[:], in0=live[g]["sums"][:], scalar1=-1.0 / D, scalar2=None, op0=ALU.mult
+                )
+            else:
                 nc.gpsimd.tensor_scalar(
                     out=neg_mean[:], in0=live[g]["sums"][:], scalar1=-1.0 / D, scalar2=0.0, op0=ALU.mult, op1=ALU.add
                 )
+            live[g]["neg_mean"] = neg_mean
+
+        def normalise(g, piece):
+            branch, j = 1 - piece // 2, piece % 2
+            if piece == 0:
+                if not TOKEN:
+                    negative_mean(g)
                 n1 = stage.tile([P, GROUP, PACK, P], F32)
                 n3 = stage.tile([P, GROUP, PACK, P], F32)
                 live[g]["normed"] = [n1, n3]
-                live[g]["neg_mean"] = neg_mean
             nc.gpsimd.tensor_scalar(
                 out=live[g]["normed"][branch][:, j, :, :],
                 in0=live[g]["pre_norm"][branch][:, j, :, :],
@@ -488,11 +498,17 @@ def tile_polymlp_skiplora_pa_t_kernel(
             for c in range(CHUNKS):
                 if UNPACK_SLOT[c] + QX_LAG == slot:
                     quantise_x(c)
+            at = piece_at(slot - LAG_GATE)
+            if TOKEN and at and at[1] == GROUP:
+                quantise_h(at[0])
+            at = piece_at(slot - LAG_N)
+            if TOKEN and at and at[1] == 0:
+                negative_mean(at[0])
             at = piece_at(slot)
             if at:
                 add_first_bias(*at)
             at = piece_at(slot - LAG_GATE)
-            if at and at[1] == GROUP:
+            if not TOKEN and at and at[1] == GROUP:
                 quantise_h(at[0])
             at = piece_at(slot - LAG_SQ)
             if at:

@@ -19,32 +19,45 @@ D = 512
 DQ = 128
 EPS = 1e-6
 TILES = TOKENS // P
-GROUP = 2
-GROUPS = TILES // GROUP
-PIECES = 2 * GROUP
 CHUNK_TILES = [2, 2] + [4] * 7
 CHUNK_START = [sum(CHUNK_TILES[:c]) for c in range(len(CHUNK_TILES))]
 CHUNKS = len(CHUNK_TILES)
+HEAD1 = 0
+TAIL1 = 0
+SIZES = [1] * HEAD1 + [2] * ((TILES - HEAD1 - TAIL1) // 2) + [1] * TAIL1
+GROUPS = len(SIZES)
+FIRST_TILE = [sum(SIZES[:g]) for g in range(GROUPS)]
+START = [2 * t for t in FIRST_TILE]
 
 AHEAD_F = 2
-LAG_SQ = 2
-LAG_N = 6
-LAG_T = 8
-LAG_EV = 9
-LAG_GATE = 12
-LAG_L = 15
-LAG_FI = 19
-UNPACK_SLOT = [-6, -5, -4, -3, -2, -1, 0, 1, 2]
-QX_LAG = 4
-X_ON_VECTOR = [0, 0, 0, 0, 0, 0, 0, 0, 0]
-N_FIRST, N_TURN, N_LAST = 3, 3, 2
-OWN = False
-SCALAR_FROM = 3
-PRE_BUFS, OUT_BUFS = 5, 3
-CONST_A_SLOT, CONST_B_SLOT, CONST_C_SLOT = -6, -6, 5
-STORE_BY_TILE = 1
-TOKEN = 1
-SCALAR_PIECE = 3
+SQ = [0, 2, 2]
+NRM = [0, 4, 6]
+TRN = [0, 6, 8]
+EV = [0, 7, 9]
+GATE = [0, 9, 12]
+QH = [0, 11, 14]
+LAST = [0, 12, 15]
+ADD = [0, 15, 19]
+UNPACK_SLOT = [-5, -3, -1, 1, 3, 4, 5, 6, 7]
+QX_LAG = 2
+X_ON_VECTOR = [0] * 9
+N_FIRST = 3
+N_TURN = 3
+N_LAST = 2
+SCALAR_FROM = 6
+PRE_BUFS = 5
+OUT_BUFS = 3
+CONST_A_SLOT = -4
+CONST_B_SLOT = 3
+CONST_C_SLOT = 5
+NORM_V_FROM = 99
+LATE = 0
+LSTEP = 1
+LAST_LATE = 15
+ADD_LATE = 16
+LRANK = 12
+ARANK = 0
+QSPLIT = 0
 
 FLOPS = 2 * TOKENS * D * D * 2 + 2 * TOKENS * DQ * D
 
@@ -94,27 +107,41 @@ def tile_polymlp_skiplora_pa_t_kernel(
         keep = ctx.enter_context(tc.tile_pool(name="keep", bufs=1))
         x_in = ctx.enter_context(tc.tile_pool(name="x_in", bufs=CHUNKS))
         stage = ctx.enter_context(tc.tile_pool(name="stage", bufs=2))
+        normed_pool = ctx.enter_context(tc.tile_pool(name="normed_pool", bufs=3))
         scaled_pool = ctx.enter_context(tc.tile_pool(name="scaled_pool", bufs=OUT_BUFS))
-        x_stage = ctx.enter_context(tc.tile_pool(name="x_stage", bufs=4))
+        x_stage = ctx.enter_context(tc.tile_pool(name="x_stage", bufs=5))
         pre_pool = ctx.enter_context(tc.tile_pool(name="pre_pool", bufs=PRE_BUFS))
         small = ctx.enter_context(tc.tile_pool(name="small", bufs=PRE_BUFS + 2))
-        results = ctx.enter_context(tc.tile_pool(name="results", bufs=3))
+        results = ctx.enter_context(tc.tile_pool(name="results", bufs=5))
         psum_first = ctx.enter_context(tc.psum_pool(name="psum_first", bufs=N_FIRST))
-        psum_own = ctx.enter_context(tc.psum_pool(name="psum_own", bufs=1)) if OWN else None
         psum_turn = ctx.enter_context(tc.psum_pool(name="psum_turn", bufs=N_TURN))
         psum_last = ctx.enter_context(tc.psum_pool(name="psum_last", bufs=N_LAST))
         ctx.enter_context(tc.manual_schedule())
 
         eps = consts.tile([P, 1], F32)
         nc.vector.memset(eps[:], EPS)
-        table_warm = consts.tile([P, 1], F32)
-        nc.scalar.activation(out=table_warm[:], in_=eps[:], func=ACT.Abs_reciprocal_sqrt)
-
         ident_f32 = consts.tile([P, P], F32)
         make_identity(nc, ident_f32[:])
         ident_bf16 = consts.tile([P, P], BF16)
         make_identity(nc, ident_bf16[:])
 
+        def load_by_feature(vec, name):
+            column = consts.tile([P, PACK], BF16, name=name)
+            nc.gpsimd.dma_start(out=column[:], in_=vec.rearrange("(m t) -> m t", t=PACK))
+            return column
+
+        with nc.allow_non_contiguous_dma(reason="four neighbouring elements of a 512-vector to a partition"):
+            u1b_raw = load_by_feature(U1_b, "u1b_raw")
+            u3b_raw = load_by_feature(U3_b, "u3b_raw")
+            g1_raw = load_by_feature(ln1_g, "g1_raw")
+            b1_raw = load_by_feature(ln1_b, "b1_raw")
+            g3_raw = load_by_feature(ln3_g, "g3_raw")
+            b3_raw = load_by_feature(ln3_b, "b3_raw")
+            alpha_raw = consts.tile([P, 1], BF16)
+            nc.gpsimd.dma_start(out=alpha_raw[:], in_=alpha.partition_broadcast(P))
+            cb_raw = load_by_feature(C_b, "cb_raw")
+
+        u3_rows = consts.tile([P, PACK, DQ], BF16)
         x_chunks = []
         z_chunks = []
         for c in range(CHUNKS):
@@ -122,35 +149,22 @@ def tile_polymlp_skiplora_pa_t_kernel(
             x_chunk = x_in.tile([P, CHUNK_TILES[c], D], BF16)
             nc.sync.dma_start(out=x_chunk[:], in_=x_view[:, tiles, :])
             x_chunks.append(x_chunk)
+            if c == 0:
+                w1_codes, w1_plane = load_mx_weight(nc, consts, U1_w_words, U1_w_scales, "w1")
             z_chunk = x_in.tile([P, CHUNK_TILES[c], DQ], BF16)
             nc.sync.dma_start(out=z_chunk[:], in_=z_view[:, tiles, :])
             z_chunks.append(z_chunk)
             if c == 0:
-                w1_codes, w1_plane = load_mx_weight(nc, consts, U1_w_words, U1_w_scales, "w1")
-        c_codes, c_plane = load_mx_weight(nc, consts, C_w_words, C_w_scales, "c")
+                nc.sync.dma_start(out=u3_rows[:], in_=U3_w.rearrange("(m t) k -> m t k", t=PACK))
+            if c == 3:
+                c_codes, c_plane = load_mx_weight(nc, consts, C_w_words, C_w_scales, "c")
 
-        u3_rows = consts.tile([P, PACK, DQ], BF16)
-        nc.scalar.dma_start(out=u3_rows[:], in_=U3_w.rearrange("(m t) k -> m t k", t=PACK))
+        table_warm = consts.tile([P, 1], F32)
+        nc.scalar.activation(out=table_warm[:], in_=eps[:], func=ACT.Abs_reciprocal_sqrt)
 
         first_row = consts.tile([P, P], BF16)
         nc.vector.memset(first_row[:], 0.0)
         nc.vector.memset(first_row[0:1, :], 1.0)
-
-        def load_by_feature(vec, name):
-            column = consts.tile([P, PACK], BF16, name=name)
-            nc.scalar.dma_start(out=column[:], in_=vec.rearrange("(m t) -> m t", t=PACK))
-            return column
-
-        with nc.allow_non_contiguous_dma(reason="four neighbouring elements of a 512-vector to a partition"):
-            u1b_raw = load_by_feature(U1_b, "u1b_raw")
-            u3b_raw = load_by_feature(U3_b, "u3b_raw")
-            cb_raw = load_by_feature(C_b, "cb_raw")
-            g1_raw = load_by_feature(ln1_g, "g1_raw")
-            b1_raw = load_by_feature(ln1_b, "b1_raw")
-            g3_raw = load_by_feature(ln3_g, "g3_raw")
-            b3_raw = load_by_feature(ln3_b, "b3_raw")
-            alpha_raw = consts.tile([P, 1], BF16)
-            nc.scalar.dma_start(out=alpha_raw[:], in_=alpha.partition_broadcast(P))
 
         xq_codes = keep.tile([P, TOKENS], U32, align_bytes=64)
         xq_plane = keep.tile([P, TOKENS], U8, align_bytes=64)
@@ -196,17 +210,10 @@ def tile_polymlp_skiplora_pa_t_kernel(
                 in_=grouped_x[c][:, 0 : P * CHUNK_TILES[c], :].rearrange("p w t -> p (w t)"),
             )
 
-        const = {}
-
-        def as_f32(raw, name):
-            column = consts.tile([P, PACK], F32, name=name)
-            nc.gpsimd.tensor_copy(out=column[:], in_=raw[:])
-            return column
-
-        def spread(column):
-            bank = psum_turn.tile([P, PACK, P], F32, tag="turn")
+        def spread(column, ident, dtype):
+            bank = psum_turn.tile([P, PACK, P], dtype, tag="turn")
             for t in range(PACK):
-                nc.tensor.transpose(bank[:, t, :], column[:, t : t + 1].to_broadcast([P, P]), ident_f32[:])
+                nc.tensor.transpose(bank[:, t, :], column[:, t : t + 1].to_broadcast([P, P]), ident[:])
             return bank
 
         u3T = consts.tile([P, PACK, P], BF16)
@@ -218,31 +225,32 @@ def tile_polymlp_skiplora_pa_t_kernel(
         gate_gain = consts.tile([P, PACK], F32)
         gate_shift = consts.tile([P, PACK], F32)
         offset1_spread = consts.tile([P, PACK, P], F32)
+        offset1 = consts.tile([P, PACK], F32)
 
         def constants_of_the_first_matmuls():
+            nc.vector.tensor_copy(out=bias1[:], in_=spread(u1b_raw, ident_bf16, BF16)[:])
             u3T_bank = psum_last.tile([P, PACK, P], BF16, tag="last")
             for t in range(PACK):
                 nc.tensor.transpose(u3T_bank[:, t, :], u3_rows[:, t, :], ident_bf16[:])
             nc.vector.tensor_copy(out=u3T[:], in_=u3T_bank[:])
-            nc.vector.tensor_copy(out=bias1[:], in_=spread(as_f32(u1b_raw, "u1b"))[:])
-            bias3_bank = spread(as_f32(u3b_raw, "u3b"))
+            bias3_bank = spread(u3b_raw, ident_bf16, BF16)
             nc.vector.tensor_copy(out=bias3[:], in_=bias3_bank[:])
             nc.vector.tensor_copy(out=bias3_rows[:], in_=bias3_bank[:])
 
-        offset1 = consts.tile([P, PACK], F32)
-
         def spreads_of_the_gate():
+            nc.vector.tensor_copy(out=offset1_spread[:], in_=spread(offset1, ident_f32, F32)[:])
             nc.vector.tensor_copy(
                 out=bias_out[:].rearrange("p (m t) -> p m t", t=PACK),
-                in_=spread(as_f32(cb_raw, "cb"))[:].rearrange("p t m -> p m t"),
+                in_=spread(cb_raw, ident_bf16, BF16)[:].rearrange("p t m -> p m t"),
             )
-            nc.vector.tensor_copy(out=offset1_spread[:], in_=spread(offset1)[:])
 
         def constants_of_the_gate():
             alpha_f32 = consts.tile([P, 1], F32)
             nc.gpsimd.tensor_copy(out=alpha_f32[:], in_=alpha_raw[:])
-            gain1 = as_f32(g1_raw, "gain1")
-            shift1 = as_f32(b1_raw, "shift1")
+            affine1 = consts.tile([P, 2, PACK], F32)
+            nc.gpsimd.tensor_copy(out=affine1[:, 0, :], in_=g1_raw[:])
+            nc.gpsimd.tensor_copy(out=affine1[:, 1, :], in_=b1_raw[:])
+            gain1, shift1 = affine1[:, 0, :], affine1[:, 1, :]
             gain3 = consts.tile([P, PACK], F32)
             nc.gpsimd.tensor_scalar(
                 out=gain3[:], in0=g3_raw[:], scalar1=alpha_f32[:, 0:1], scalar2=None, op0=ALU.mult
@@ -251,42 +259,39 @@ def tile_polymlp_skiplora_pa_t_kernel(
             nc.gpsimd.tensor_scalar(
                 out=shift3[:], in0=b3_raw[:], scalar1=alpha_f32[:, 0:1], scalar2=1.0, op0=ALU.mult, op1=ALU.add
             )
-
-            def small_tile(name):
-                return consts.tile([P, PACK], F32, name=name)
-
-            def magnitude(column, name):
-                negative = small_tile(name + "_neg")
-                nc.vector.tensor_scalar(out=negative[:], in0=column[:], scalar1=-1.0, scalar2=None, op0=ALU.mult)
-                result = small_tile(name)
-                nc.vector.tensor_tensor(out=result[:], in0=column[:], in1=negative[:], op=ALU.max)
-                return result
-
-            floor1 = small_tile("floor1")
+            negative = consts.tile([P, 2, PACK], F32)
+            nc.vector.tensor_scalar(out=negative[:], in0=affine1[:], scalar1=-1.0, scalar2=None, op0=ALU.mult)
+            magnitude = consts.tile([P, 2, PACK], F32)
+            nc.vector.tensor_tensor(out=magnitude[:], in0=affine1[:], in1=negative[:], op=ALU.max)
+            floor1 = consts.tile([P, PACK], F32)
             nc.vector.tensor_scalar(
-                out=floor1[:], in0=magnitude(shift1, "abs_shift1")[:], scalar1=2.0**-100, scalar2=2.0**-126,
+                out=floor1[:], in0=magnitude[:, 1, :], scalar1=2.0**-100, scalar2=2.0**-126,
                 op0=ALU.mult, op1=ALU.max,
             )
-            large_enough = small_tile("large_enough")
-            nc.vector.tensor_tensor(out=large_enough[:], in0=magnitude(gain1, "abs_gain1")[:], in1=floor1[:], op=ALU.is_ge)
-            safe_gain = small_tile("safe_gain")
-            nc.vector.tensor_tensor(out=safe_gain[:], in0=gain1[:], in1=floor1[:], op=ALU.subtract)
+            large_enough = consts.tile([P, PACK], F32)
+            nc.vector.tensor_tensor(out=large_enough[:], in0=magnitude[:, 0, :], in1=floor1[:], op=ALU.is_ge)
+            safe_gain = consts.tile([P, PACK], F32)
+            nc.vector.tensor_tensor(out=safe_gain[:], in0=gain1, in1=floor1[:], op=ALU.subtract)
             nc.vector.tensor_tensor(out=safe_gain[:], in0=safe_gain[:], in1=large_enough[:], op=ALU.mult)
             nc.vector.tensor_tensor(out=safe_gain[:], in0=safe_gain[:], in1=floor1[:], op=ALU.add)
             nc.vector.reciprocal(out=offset1[:], in_=safe_gain[:])
-            nc.vector.tensor_tensor(out=offset1[:], in0=offset1[:], in1=shift1[:], op=ALU.mult)
-            nc.vector.tensor_tensor(out=gate_gain[:], in0=safe_gain[:], in1=gain3[:], op=ALU.mult)
-            nc.vector.tensor_tensor(out=gate_shift[:], in0=safe_gain[:], in1=shift3[:], op=ALU.mult)
+            nc.vector.tensor_tensor(out=offset1[:], in0=offset1[:], in1=shift1, op=ALU.mult)
+            nc.gpsimd.tensor_tensor(out=gate_gain[:], in0=safe_gain[:], in1=gain3[:], op=ALU.mult)
+            nc.gpsimd.tensor_tensor(out=gate_shift[:], in0=safe_gain[:], in1=shift3[:], op=ALU.mult)
 
         live = {}
 
+        def group_state(g):
+            return live.setdefault(g, {})
+
+        def on_scalar(tile):
+            return tile % 2 == 1 and tile >= SCALAR_FROM
+
         def first_matmul(g, piece):
             j, branch = divmod(piece, 2)
-            cols = slice(P * (GROUP * g + j), P * (GROUP * g + j + 1))
-            if piece == SCALAR_PIECE and g >= SCALAR_FROM and OWN:
-                acc = psum_own.tile([P, D], F32, tag="own")
-            else:
-                acc = psum_first.tile([P, D], F32, tag="first")
+            tile = FIRST_TILE[g] + j
+            cols = slice(P * tile, P * (tile + 1))
+            acc = psum_first.tile([P, D], F32, tag="first")
             if branch == 0:
                 nc.tensor.matmul_mx(
                     out=acc[:],
@@ -299,7 +304,7 @@ def tile_polymlp_skiplora_pa_t_kernel(
                 )
                 by_feature_tile = acc[:].rearrange("p (m t) -> p t m", t=PACK)
             else:
-                if piece == SCALAR_PIECE and g >= SCALAR_FROM:
+                if on_scalar(tile):
                     nc.tensor.matmul(
                         out=acc[:],
                         lhsT=first_row[:],
@@ -311,105 +316,105 @@ def tile_polymlp_skiplora_pa_t_kernel(
                     out=acc[:],
                     lhsT=z2T[:, cols],
                     rhs=u3T[:].rearrange("k t m -> k (t m)"),
-                    start=not (piece == SCALAR_PIECE and g >= SCALAR_FROM),
+                    start=not on_scalar(tile),
                     stop=True,
                 )
                 by_feature_tile = acc[:].rearrange("p (t m) -> p t m", t=PACK)
-            live.setdefault(g, {})[("first", piece)] = by_feature_tile
+            group_state(g)[("first", piece)] = by_feature_tile
 
         def add_first_bias(g, piece):
             j, branch = divmod(piece, 2)
+            s = live[g]
             if piece == 0:
-                y1 = pre_pool.tile([P, GROUP, PACK, P], F32)
-                y3 = pre_pool.tile([P, GROUP, PACK, P], F32)
-                sums = small.tile([P, 2, GROUP], F32)
-                live[g]["pre_norm"] = [y1, y3]
-                live[g]["sums"] = sums
-            if piece == SCALAR_PIECE and g >= SCALAR_FROM:
+                y1 = pre_pool.tile([P, 2, PACK, P], F32)
+                y3 = pre_pool.tile([P, 2, PACK, P], F32)
+                sums = small.tile([P, 2, 2], F32)
+                s["pre_norm"] = [y1, y3]
+                s["sums"] = sums
+            if branch == 1 and on_scalar(FIRST_TILE[g] + j):
                 nc.scalar.activation(
-                    out=live[g]["pre_norm"][branch][:, j, :, :],
-                    in_=live[g][("first", piece)],
+                    out=s["pre_norm"][branch][:, j, :, :],
+                    in_=s[("first", piece)],
                     func=ACT.Identity,
-                    accum_out=live[g]["sums"][:, branch, j : j + 1],
+                    accum_out=s["sums"][:, branch, j : j + 1],
                 )
                 return
             nc.vector.scalar_tensor_tensor(
-                out=live[g]["pre_norm"][branch][:, j, :, :],
-                in0=live[g][("first", piece)],
+                out=s["pre_norm"][branch][:, j, :, :],
+                in0=s[("first", piece)],
                 scalar=1.0,
                 in1=biases[branch][:],
                 op0=ALU.mult,
                 op1=ALU.add,
-                accum_out=live[g]["sums"][:, branch, j : j + 1],
+                accum_out=s["sums"][:, branch, j : j + 1],
             )
 
         def square(g, piece):
             j, branch = divmod(piece, 2)
+            s = live[g]
+            size = SIZES[g]
             if piece == 0:
-                square_sums = small.tile([P, 2, GROUP], F32)
-                live[g]["square_sums"] = square_sums
+                square_sums = small.tile([P, 2, 2], F32)
+                s["square_sums"] = square_sums
             squares = stage.tile([P, D], F32)
             nc.scalar.activation(
                 out=squares[:],
-                in_=live[g]["pre_norm"][branch][:, j, :, :].rearrange("p t m -> p (t m)"),
+                in_=s["pre_norm"][branch][:, j, :, :].rearrange("p t m -> p (t m)"),
                 func=ACT.Square,
-                bias=live[g]["sums"][:, branch, j : j + 1],
+                bias=s["sums"][:, branch, j : j + 1],
                 scale=-float(D),
-                accum_out=live[g]["square_sums"][:, branch, j : j + 1],
+                accum_out=s["square_sums"][:, branch, j : j + 1],
             )
-            if piece == PIECES - 1:
-                rstd = small.tile([P, 2, GROUP], F32)
+            if piece == 2 * size - 1:
+                rstd = small.tile([P, 2, 2], F32)
                 nc.scalar.activation(
-                    out=rstd[:],
-                    in_=live[g]["square_sums"][:],
+                    out=rstd[:, :, 0:size],
+                    in_=s["square_sums"][:, :, 0:size],
                     func=ACT.Abs_reciprocal_sqrt,
                     bias=eps[:, 0:1],
                     scale=1.0 / D**3,
                 )
-                live[g]["rstd"] = rstd
+                s["rstd"] = rstd
 
         def negative_mean(g):
-            neg_mean = small.tile([P, 2, GROUP], F32)
-            if TOKEN:
-                nc.vector.tensor_scalar(
-                    out=neg_mean[:], in0=live[g]["sums"][:], scalar1=-1.0 / D, scalar2=None, op0=ALU.mult
-                )
-            else:
-                nc.gpsimd.tensor_scalar(
-                    out=neg_mean[:], in0=live[g]["sums"][:], scalar1=-1.0 / D, scalar2=0.0, op0=ALU.mult, op1=ALU.add
-                )
+            size = SIZES[g]
+            neg_mean = small.tile([P, 2, 2], F32)
+            nc.vector.tensor_scalar(
+                out=neg_mean[:, :, 0:size], in0=live[g]["sums"][:, :, 0:size], scalar1=-1.0 / D, scalar2=None, op0=ALU.mult
+            )
             live[g]["neg_mean"] = neg_mean
 
         def normalise(g, piece):
-            branch, j = 1 - piece // 2, piece % 2
+            size = SIZES[g]
+            s = live[g]
+            branch, j = 1 - piece // size, piece % size
             if piece == 0:
-                if not TOKEN:
-                    negative_mean(g)
-                n1 = stage.tile([P, GROUP, PACK, P], F32)
-                n3 = stage.tile([P, GROUP, PACK, P], F32)
-                live[g]["normed"] = [n1, n3]
-            nc.gpsimd.tensor_scalar(
-                out=live[g]["normed"][branch][:, j, :, :],
-                in0=live[g]["pre_norm"][branch][:, j, :, :],
-                scalar1=live[g]["neg_mean"][:, branch, j : j + 1],
-                scalar2=live[g]["rstd"][:, branch, j : j + 1],
+                n1 = normed_pool.tile([P, 2, PACK, P], F32)
+                n3 = normed_pool.tile([P, 2, PACK, P], F32)
+                s["normed"] = [n1, n3]
+            (nc.vector if g >= NORM_V_FROM else nc.gpsimd).tensor_scalar(
+                out=s["normed"][branch][:, j, :, :],
+                in0=s["pre_norm"][branch][:, j, :, :],
+                scalar1=s["neg_mean"][:, branch, j : j + 1],
+                scalar2=s["rstd"][:, branch, j : j + 1],
                 op0=ALU.add,
                 op1=ALU.mult,
             )
 
         def transposes(g, piece):
-            if piece < 2:
-                pair = piece
-                nT_bank = psum_turn.tile([P, 2, GROUP * P], F32, tag="turn")
-                for s in range(2):
-                    for j in range(GROUP):
+            size = SIZES[g]
+            s = live[g]
+            if piece < size:
+                nT_bank = psum_turn.tile([P, 4 // size, size * P], F32, tag="turn")
+                for k in range(4 // size):
+                    for j in range(size):
                         nc.tensor.transpose(
-                            nT_bank[:, s, P * j : P * (j + 1)],
-                            live[g]["normed"][1][:, j, 2 * pair + s, :],
+                            nT_bank[:, k, P * j : P * (j + 1)],
+                            s["normed"][1][:, j, (4 // size) * piece + k, :],
                             ident_f32[:],
                         )
             else:
-                j = piece - 2
+                j = piece - size
                 nT_bank = psum_turn.tile([P, PACK, P], F32, tag="turn")
                 for t in range(PACK):
                     nc.tensor.matmul(
@@ -417,45 +422,51 @@ def tile_polymlp_skiplora_pa_t_kernel(
                         is_transpose=True, start=True, stop=False,
                     )
                     nc.tensor.matmul(
-                        out=nT_bank[:, t, :], lhsT=live[g]["normed"][0][:, j, t, :], rhs=ident_f32[:],
+                        out=nT_bank[:, t, :], lhsT=s["normed"][0][:, j, t, :], rhs=ident_f32[:],
                         is_transpose=True, start=False, stop=True,
                     )
-            live[g][("turned", piece)] = nT_bank
+            s[("turned", piece)] = nT_bank
 
-        def gain_and_shift(g, pair):
-            if pair == 0:
-                o3T = scaled_pool.tile([P, PACK, GROUP * P], F32)
-                live[g]["scaled"] = o3T
-            for s in range(2):
-                t = 2 * pair + s
+        def gain_and_shift(g, piece):
+            size = SIZES[g]
+            s = live[g]
+            if piece == 0:
+                o3T = scaled_pool.tile([P, PACK, 2 * P], F32)
+                s["scaled"] = o3T
+            for k in range(4 // size):
+                t = (4 // size) * piece + k
                 nc.scalar.activation(
-                    out=live[g]["scaled"][:, t, :],
-                    in_=live[g][("turned", pair)][:, s, :],
+                    out=s["scaled"][:, t, 0 : P * size],
+                    in_=s[("turned", piece)][:, k, :],
                     func=ACT.Identity,
                     bias=gate_shift[:, t : t + 1],
                     scale=gate_gain[:, t : t + 1],
                 )
 
         def gate(g, j):
+            s = live[g]
             if j == 0:
-                h_grouped = stage.tile([P, GROUP * P, PACK], BF16, align_bytes=64)
-                live[g]["h_grouped"] = h_grouped
+                h_grouped = normed_pool.tile([P, 2 * P, PACK], BF16, align_bytes=64)
+                s["h_grouped"] = h_grouped
             nc.vector.tensor_tensor(
-                out=live[g]["h_grouped"][:, P * j : P * (j + 1), :].rearrange("p (c i) t -> p c t i", i=8),
-                in0=live[g][("turned", 2 + j)][:].rearrange("p t (c i) -> p c t i", i=8),
-                in1=live[g]["scaled"][:, :, P * j : P * (j + 1)].rearrange("p t (c i) -> p c t i", i=8),
+                out=s["h_grouped"][:, P * j : P * (j + 1), :].rearrange("p (c i) t -> p c t i", i=8),
+                in0=s[("turned", SIZES[g] + j)][:].rearrange("p t (c i) -> p c t i", i=8),
+                in1=s["scaled"][:, :, P * j : P * (j + 1)].rearrange("p t (c i) -> p c t i", i=8),
                 op=ALU.mult,
             )
 
-        def quantise_h(g):
-            hq_codes = stage.tile([P, GROUP * P], U32, align_bytes=64)
-            hq_plane = stage.tile([P, GROUP * P], U8, align_bytes=64)
+        def quantise_h(g, first, count):
+            if first == 0:
+                hq_codes = normed_pool.tile([P, 2 * P], U32, align_bytes=64)
+                hq_plane = normed_pool.tile([P, 2 * P], U8, align_bytes=64)
+                live[g]["hq"] = (hq_codes, hq_plane)
+            hq_codes, hq_plane = live[g]["hq"]
+            cols = slice(P * first, P * (first + count))
             nc.vector.quantize_mx(
-                out=hq_codes[:].bitcast(FP8X4),
-                scales=hq_plane[:],
-                in_=live[g]["h_grouped"][:].rearrange("p w t -> p (w t)"),
+                out=hq_codes[:, cols].bitcast(FP8X4),
+                scales=hq_plane[:, cols],
+                in_=live[g]["h_grouped"][:, cols, :].rearrange("p w t -> p (w t)"),
             )
-            live[g]["hq"] = (hq_codes, hq_plane)
 
         def last_matmul(g, j):
             hq_codes, hq_plane = live[g]["hq"]
@@ -472,68 +483,45 @@ def tile_polymlp_skiplora_pa_t_kernel(
             live[g][("last", j)] = acc_out
 
         def add_last_bias(g, j):
-            if j == 0:
-                result = results.tile([P, GROUP, D], F32)
-                live[g]["result"] = result
-            result = live[g]["result"]
-            nc.vector.tensor_tensor(out=result[:, j, :], in0=live[g][("last", j)][:], in1=bias_out[:], op=ALU.add)
-            if STORE_BY_TILE:
-                nc.sync.dma_start(out=out_view[:, GROUP * g + j, :], in_=result[:, j, :])
-            elif j == GROUP - 1:
-                nc.sync.dma_start(out=out_view[:, GROUP * g : GROUP * (g + 1), :], in_=result[:])
+            result = results.tile([P, D], F32)
+            nc.vector.tensor_tensor(out=result[:], in0=live[g][("last", j)][:], in1=bias_out[:], op=ALU.add)
+            nc.sync.dma_start(out=out_view[:, FIRST_TILE[g] + j, :], in_=result[:])
 
-        def piece_at(slot):
-            g, piece = divmod(slot, PIECES)
-            return (g, piece) if 0 <= g < GROUPS else None
+        events = []
 
-        first_slot = min(UNPACK_SLOT)
-        for slot in range(first_slot, PIECES * GROUPS + LAG_FI + 1):
-            at = piece_at(slot - LAG_GATE)
-            if at and at[1] < GROUP:
-                gate(at[0], at[1])
-            at = piece_at(slot - LAG_FI)
-            if at and at[1] == 0:
-                for j in range(GROUP):
-                    add_last_bias(at[0], j)
-            for c in range(CHUNKS):
-                if UNPACK_SLOT[c] + QX_LAG == slot:
-                    quantise_x(c)
-            at = piece_at(slot - LAG_GATE)
-            if TOKEN and at and at[1] == GROUP:
-                quantise_h(at[0])
-            at = piece_at(slot - LAG_N)
-            if TOKEN and at and at[1] == 0:
-                negative_mean(at[0])
-            at = piece_at(slot)
-            if at:
-                add_first_bias(*at)
-            at = piece_at(slot - LAG_GATE)
-            if not TOKEN and at and at[1] == GROUP:
-                quantise_h(at[0])
-            at = piece_at(slot - LAG_SQ)
-            if at:
-                square(*at)
-            at = piece_at(slot - LAG_EV)
-            if at and at[1] < 2:
-                gain_and_shift(*at)
-            at = piece_at(slot - LAG_N)
-            if at:
-                normalise(*at)
-            at = piece_at(slot - LAG_T)
-            if at:
-                transposes(*at)
-            at = piece_at(slot + AHEAD_F)
-            if at:
-                first_matmul(*at)
-            at = piece_at(slot - LAG_L)
-            if at and at[1] < GROUP:
-                last_matmul(at[0], at[1])
-            for c in range(CHUNKS):
-                if UNPACK_SLOT[c] == slot:
-                    unpack(c)
-            if slot == CONST_A_SLOT:
-                constants_of_the_first_matmuls()
-            if slot == CONST_B_SLOT:
-                constants_of_the_gate()
-            if slot == CONST_C_SLOT:
-                spreads_of_the_gate()
+        def at(slot, rank, step, *arguments):
+            events.append((slot, rank, len(events), step, arguments))
+
+        for g in range(GROUPS):
+            size, start = SIZES[g], START[g]
+            final = g == GROUPS - 1
+            late = g >= GROUPS - LATE
+            for j in range(size):
+                at(start + GATE[size] + j, 1, gate, g, j)
+                if late:
+                    at(start + LAST_LATE + j * LSTEP, LRANK, last_matmul, g, j)
+                    at(start + ADD_LATE + j * LSTEP, ARANK, add_last_bias, g, j)
+                else:
+                    at(start + LAST[size] + j, 12, last_matmul, g, j)
+                    at(start + ADD[size], 2, add_last_bias, g, j)
+                if final and QSPLIT:
+                    at(start + GATE[size] + j, 1.5, quantise_h, g, j, 1)
+            if not (final and QSPLIT):
+                at(start + QH[size], 4, quantise_h, g, 0, size)
+            at(start + NRM[size], 5, negative_mean, g)
+            for piece in range(2 * size):
+                at(start + piece - AHEAD_F, 11, first_matmul, g, piece)
+                at(start + piece, 6, add_first_bias, g, piece)
+                at(start + SQ[size] + piece, 7, square, g, piece)
+                at(start + NRM[size] + piece, 9, normalise, g, piece)
+                at(start + TRN[size] + piece, 10, transposes, g, piece)
+            for piece in range(size):
+                at(start + EV[size] + piece, 8, gain_and_shift, g, piece)
+        for c in range(CHUNKS):
+            at(UNPACK_SLOT[c], 13, unpack, c)
+            at(UNPACK_SLOT[c] + QX_LAG, 3, quantise_x, c)
+        at(CONST_A_SLOT, 14, constants_of_the_first_matmuls)
+        at(CONST_B_SLOT, 14, constants_of_the_gate)
+        at(CONST_C_SLOT, 14, spreads_of_the_gate)
+        for event in sorted(events, key=lambda e: e[:3]):
+            event[3](*event[4])

@@ -38,8 +38,8 @@ GATE = [0, 9, 12]
 QH = [0, 11, 14]
 LAST = [0, 12, 15]
 ADD = [0, 15, 19]
-UNPACK_SLOT = [-5, -3, -1, 1, 3, 4, 5, 6, 7]
-QX_LAG = 2
+UNPACK_SLOT = [-6, -5, -4, -3, -2, -1, 0, 1, 2]
+QX_LAG = 4
 X_ON_VECTOR = [0] * 9
 N_FIRST = 3
 N_TURN = 3
@@ -47,11 +47,13 @@ N_LAST = 2
 SCALAR_FROM = 6
 PRE_BUFS = 5
 OUT_BUFS = 3
-CONST_A_SLOT = -4
+CONST_A_SLOT = -6
 CONST_B_SLOT = 3
 CONST_C_SLOT = 5
 NORM_V_FROM = 99
 LATE = 0
+XPOOL = [0] * 9
+ZPOOL = [1] * 9
 LSTEP = 1
 LAST_LATE = 15
 ADD_LATE = 16
@@ -120,26 +122,25 @@ def tile_polymlp_skiplora_pa_t_kernel(
 
         eps = consts.tile([P, 1], F32)
         nc.vector.memset(eps[:], EPS)
-        ident_f32 = consts.tile([P, P], F32)
-        make_identity(nc, ident_f32[:])
-        ident_bf16 = consts.tile([P, P], BF16)
-        make_identity(nc, ident_bf16[:])
-
-        def load_by_feature(vec, name):
+        def load_by_feature(queue, vec, name):
             column = consts.tile([P, PACK], BF16, name=name)
-            nc.gpsimd.dma_start(out=column[:], in_=vec.rearrange("(m t) -> m t", t=PACK))
+            queue.dma_start(out=column[:], in_=vec.rearrange("(m t) -> m t", t=PACK))
             return column
 
         with nc.allow_non_contiguous_dma(reason="four neighbouring elements of a 512-vector to a partition"):
-            u1b_raw = load_by_feature(U1_b, "u1b_raw")
-            u3b_raw = load_by_feature(U3_b, "u3b_raw")
-            g1_raw = load_by_feature(ln1_g, "g1_raw")
-            b1_raw = load_by_feature(ln1_b, "b1_raw")
-            g3_raw = load_by_feature(ln3_g, "g3_raw")
-            b3_raw = load_by_feature(ln3_b, "b3_raw")
+            u1b_raw = load_by_feature(nc.scalar, U1_b, "u1b_raw")
+            u3b_raw = load_by_feature(nc.scalar, U3_b, "u3b_raw")
+            ident_f32 = consts.tile([P, P], F32)
+            make_identity(nc, ident_f32[:])
+            ident_bf16 = consts.tile([P, P], BF16)
+            make_identity(nc, ident_bf16[:])
+            g1_raw = load_by_feature(nc.gpsimd, ln1_g, "g1_raw")
+            b1_raw = load_by_feature(nc.gpsimd, ln1_b, "b1_raw")
+            g3_raw = load_by_feature(nc.gpsimd, ln3_g, "g3_raw")
+            b3_raw = load_by_feature(nc.gpsimd, ln3_b, "b3_raw")
             alpha_raw = consts.tile([P, 1], BF16)
             nc.gpsimd.dma_start(out=alpha_raw[:], in_=alpha.partition_broadcast(P))
-            cb_raw = load_by_feature(C_b, "cb_raw")
+            cb_raw = load_by_feature(nc.gpsimd, C_b, "cb_raw")
 
         u3_rows = consts.tile([P, PACK, DQ], BF16)
         x_chunks = []
@@ -181,7 +182,8 @@ def tile_polymlp_skiplora_pa_t_kernel(
             x_grouped = x_stage.tile([P, 4 * P, PACK], BF16, align_bytes=64)
             grouped_words = x_grouped[:].rearrange("p w t -> p (w t)").bitcast(F32)
             for half in range(n_tiles // 2):
-                xT_bank = psum_turn.tile([P, 2, 2, P], F32, tag="turn")
+                pool, tag = (psum_last, "last") if XPOOL[c] else (psum_turn, "turn")
+                xT_bank = pool.tile([P, 2, 2, P], F32, tag=tag)
                 for i in range(2):
                     first = words_per_tile * (2 * half + i)
                     for u in range(2):
@@ -198,7 +200,8 @@ def tile_polymlp_skiplora_pa_t_kernel(
                     in_=xT_bank[:].rearrange("p i u w -> p i w u"),
                 )
             grouped_x[c] = x_grouped
-            zT_bank = psum_last.tile([P, n_tiles, P], BF16, tag="last")
+            pool, tag = (psum_last, "last") if ZPOOL[c] else (psum_turn, "turn")
+            zT_bank = pool.tile([P, n_tiles, P], BF16, tag=tag)
             for i in range(n_tiles):
                 nc.tensor.transpose(zT_bank[:, i, :], z_chunks[c][:, i, :], ident_bf16[:])
             nc.scalar.copy(out=z2T[:, chunk_columns(c)], in_=zT_bank[:].rearrange("p i w -> p (i w)"))

@@ -48,18 +48,24 @@ SCALAR_FROM = 6
 PRE_BUFS = 5
 OUT_BUFS = 3
 CONST_A_SLOT = -6
-CONST_B_SLOT = 3
+CONST_B_SLOT = 0
 CONST_C_SLOT = 5
-NORM_V_FROM = 99
-LATE = 0
+NORM_V = ()
+Z_LOADS = [(c, CHUNK_START[c], CHUNK_TILES[c]) for c in range(CHUNKS)]
+U3_AT = 0
+C_AT = 8
+NRM_FINAL = 6
+NSTEP = 1
+RRANK = 8.5
+LATE = 2
 XPOOL = [0] * 9
 ZPOOL = [1] * 9
 LSTEP = 1
 LAST_LATE = 15
 ADD_LATE = 16
-LRANK = 12
-ARANK = 0
-QSPLIT = 0
+LRANK = 9
+ARANK = 1.2
+QSPLIT = 1
 
 FLOPS = 2 * TOKENS * D * D * 2 + 2 * TOKENS * DQ * D
 
@@ -108,6 +114,7 @@ def tile_polymlp_skiplora_pa_t_kernel(
         consts = ctx.enter_context(tc.tile_pool(name="consts", bufs=1))
         keep = ctx.enter_context(tc.tile_pool(name="keep", bufs=1))
         x_in = ctx.enter_context(tc.tile_pool(name="x_in", bufs=CHUNKS))
+        z_in = ctx.enter_context(tc.tile_pool(name="z_in", bufs=1))
         stage = ctx.enter_context(tc.tile_pool(name="stage", bufs=2))
         normed_pool = ctx.enter_context(tc.tile_pool(name="normed_pool", bufs=3))
         scaled_pool = ctx.enter_context(tc.tile_pool(name="scaled_pool", bufs=OUT_BUFS))
@@ -144,7 +151,7 @@ def tile_polymlp_skiplora_pa_t_kernel(
 
         u3_rows = consts.tile([P, PACK, DQ], BF16)
         x_chunks = []
-        z_chunks = []
+        z_tiles = {}
         for c in range(CHUNKS):
             tiles = slice(CHUNK_START[c], CHUNK_START[c] + CHUNK_TILES[c])
             x_chunk = x_in.tile([P, CHUNK_TILES[c], D], BF16)
@@ -152,12 +159,15 @@ def tile_polymlp_skiplora_pa_t_kernel(
             x_chunks.append(x_chunk)
             if c == 0:
                 w1_codes, w1_plane = load_mx_weight(nc, consts, U1_w_words, U1_w_scales, "w1")
-            z_chunk = x_in.tile([P, CHUNK_TILES[c], DQ], BF16)
-            nc.sync.dma_start(out=z_chunk[:], in_=z_view[:, tiles, :])
-            z_chunks.append(z_chunk)
-            if c == 0:
+            for before, first, count in Z_LOADS:
+                if before == c:
+                    z_part = z_in.tile([P, count, DQ], BF16, name="z_part_%d" % first)
+                    nc.sync.dma_start(out=z_part[:], in_=z_view[:, first : first + count, :])
+                    for i in range(count):
+                        z_tiles[first + i] = z_part[:, i, :]
+            if c == U3_AT:
                 nc.sync.dma_start(out=u3_rows[:], in_=U3_w.rearrange("(m t) k -> m t k", t=PACK))
-            if c == 3:
+            if c == C_AT:
                 c_codes, c_plane = load_mx_weight(nc, consts, C_w_words, C_w_scales, "c")
 
         table_warm = consts.tile([P, 1], F32)
@@ -203,7 +213,7 @@ def tile_polymlp_skiplora_pa_t_kernel(
             pool, tag = (psum_last, "last") if ZPOOL[c] else (psum_turn, "turn")
             zT_bank = pool.tile([P, n_tiles, P], BF16, tag=tag)
             for i in range(n_tiles):
-                nc.tensor.transpose(zT_bank[:, i, :], z_chunks[c][:, i, :], ident_bf16[:])
+                nc.tensor.transpose(zT_bank[:, i, :], z_tiles[CHUNK_START[c] + i], ident_bf16[:])
             nc.scalar.copy(out=z2T[:, chunk_columns(c)], in_=zT_bank[:].rearrange("p i w -> p (i w)"))
 
         def quantise_x(c):
@@ -368,16 +378,18 @@ def tile_polymlp_skiplora_pa_t_kernel(
                 scale=-float(D),
                 accum_out=s["square_sums"][:, branch, j : j + 1],
             )
-            if piece == 2 * size - 1:
-                rstd = small.tile([P, 2, 2], F32)
-                nc.scalar.activation(
-                    out=rstd[:, :, 0:size],
-                    in_=s["square_sums"][:, :, 0:size],
-                    func=ACT.Abs_reciprocal_sqrt,
-                    bias=eps[:, 0:1],
-                    scale=1.0 / D**3,
-                )
-                s["rstd"] = rstd
+
+        def reciprocal_deviation(g):
+            size = SIZES[g]
+            rstd = small.tile([P, 2, 2], F32)
+            nc.scalar.activation(
+                out=rstd[:, :, 0:size],
+                in_=live[g]["square_sums"][:, :, 0:size],
+                func=ACT.Abs_reciprocal_sqrt,
+                bias=eps[:, 0:1],
+                scale=1.0 / D**3,
+            )
+            live[g]["rstd"] = rstd
 
         def negative_mean(g):
             size = SIZES[g]
@@ -395,7 +407,7 @@ def tile_polymlp_skiplora_pa_t_kernel(
                 n1 = normed_pool.tile([P, 2, PACK, P], F32)
                 n3 = normed_pool.tile([P, 2, PACK, P], F32)
                 s["normed"] = [n1, n3]
-            (nc.vector if g >= NORM_V_FROM else nc.gpsimd).tensor_scalar(
+            (nc.vector if g == GROUPS - 1 and piece in NORM_V else nc.gpsimd).tensor_scalar(
                 out=s["normed"][branch][:, j, :, :],
                 in0=s["pre_norm"][branch][:, j, :, :],
                 scalar1=s["neg_mean"][:, branch, j : j + 1],
@@ -512,11 +524,12 @@ def tile_polymlp_skiplora_pa_t_kernel(
             if not (final and QSPLIT):
                 at(start + QH[size], 4, quantise_h, g, 0, size)
             at(start + NRM[size], 5, negative_mean, g)
+            at(start + SQ[size] + 2 * size - 1, RRANK, reciprocal_deviation, g)
             for piece in range(2 * size):
                 at(start + piece - AHEAD_F, 11, first_matmul, g, piece)
                 at(start + piece, 6, add_first_bias, g, piece)
                 at(start + SQ[size] + piece, 7, square, g, piece)
-                at(start + NRM[size] + piece, 9, normalise, g, piece)
+                at(start + (NRM[size] if not final else NRM_FINAL) + piece * (1 if not final else NSTEP), 9, normalise, g, piece)
                 at(start + TRN[size] + piece, 10, transposes, g, piece)
             for piece in range(size):
                 at(start + EV[size] + piece, 8, gain_and_shift, g, piece)

from contextlib import ExitStack

import concourse.mybir as mybir
from concourse.masks import make_identity

F32 = mybir.dt.float32
BF16 = mybir.dt.bfloat16
I32 = mybir.dt.int32
U32 = mybir.dt.uint32
U8 = mybir.dt.uint8
FP8X4 = mybir.dt.float8_e4m3fn_x4
ALU = mybir.AluOpType
ACT = mybir.ActivationFunctionType

P = 128
PACK = 4
TOKENS = 16 * 16 * 16
D = 512
DQ = 128
EPS = 1e-6
TILES = TOKENS // P
CHUNK_TILES = [2, 2] + [4] * 7
CHUNK_START = [sum(CHUNK_TILES[:c]) for c in range(len(CHUNK_TILES))]
CHUNKS = len(CHUNK_TILES)
HEAD1 = 0
TAIL1 = 0
SIZES = [1] * HEAD1 + [2] * ((TILES - HEAD1 - TAIL1) // 2) + [1] * TAIL1
GROUPS = len(SIZES)
FIRST_TILE = [sum(SIZES[:g]) for g in range(GROUPS)]
START = [2 * t for t in FIRST_TILE]

AHEAD_F = 2
SQ = [0, 2, 2]
NRM = [0, 4, 6]
TRN = [0, 6, 8]
EV = [0, 7, 9]
GATE = [0, 9, 12]
QH = [0, 11, 14]
LAST = [0, 12, 15]
ADD = [0, 15, 19]
UNPACK_SLOT = [-6, -5, -4, -3, -2, -1, 0, 1, 2]
QX_LAG = 4
X_ON_VECTOR = [0] * 9
N_FIRST = 3
N_TURN = 3
N_LAST = 2
SCALAR_FROM = 6
PRE_BUFS = 5
OUT_BUFS = 3
CONST_A_SLOT = -6
CONST_B_SLOT = 0
CONST_C_SLOT = 5
NORM_V = ()
Z_LOADS = [(c, CHUNK_START[c], CHUNK_TILES[c]) for c in range(CHUNKS)]
U3_AT = 0
C_AT = 8
NRM_FINAL = 6
NSTEP = 1
RRANK = 8.5
LATE = 2
XPOOL = [0] * 9
ZPOOL = [1] * 9
LSTEP = 1
LAST_LATE = 15
ADD_LATE = 16
LRANK = 9
ARANK = 1.2
QSPLIT = 1

FLOPS = 2 * TOKENS * D * D * 2 + 2 * TOKENS * DQ * D


def load_mx_weight(nc, pool, words, scales, name):
    codes = pool.tile([P, PACK * D], U8, name=name + "_codes", align_bytes=64)
    plane = pool.tile([P, D], U8, name=name + "_plane", align_bytes=64)
    nc.vector.memset(plane[:].bitcast(I32), 0)
    for quadrant in range(4):
        nc.sync.dma_start(
            out=plane[32 * quadrant : 32 * quadrant + 4, :].bitcast(I32),
            in_=scales[0, 4 * quadrant : 4 * quadrant + 4, :].bitcast(I32),
        )
    nc.sync.dma_start(
        out=codes[:].bitcast(I32),
        in_=words[0].rearrange("p n t -> p (n t)").bitcast(I32),
    )
    return codes, plane


def tile_polymlp_skiplora_pa_t_kernel(
    tc,
    x,
    z2,
    U1_w_words,
    U1_w_scales,
    U1_b,
    U3_w,
    U3_b,
    C_w_words,
    C_w_scales,
    C_b,
    ln1_g,
    ln1_b,
    ln3_g,
    ln3_b,
    alpha,
    out,
):
    nc = tc.nc
    x_view = x.flatten_outer_dims().rearrange("(p i) d -> p i d", i=TILES)
    z_view = z2.flatten_outer_dims().rearrange("(p i) d -> p i d", i=TILES)
    out_view = out.flatten_outer_dims().rearrange("(p i) d -> p i d", i=TILES)

    with ExitStack() as ctx:
        consts = ctx.enter_context(tc.tile_pool(name="consts", bufs=1))
        keep = ctx.enter_context(tc.tile_pool(name="keep", bufs=1))
        x_in = ctx.enter_context(tc.tile_pool(name="x_in", bufs=CHUNKS))
        z_in = ctx.enter_context(tc.tile_pool(name="z_in", bufs=1))
        stage = ctx.enter_context(tc.tile_pool(name="stage", bufs=2))
        normed_pool = ctx.enter_context(tc.tile_pool(name="normed_pool", bufs=3))
        scaled_pool = ctx.enter_context(tc.tile_pool(name="scaled_pool", bufs=OUT_BUFS))
        x_stage = ctx.enter_context(tc.tile_pool(name="x_stage", bufs=5))
        pre_pool = ctx.enter_context(tc.tile_pool(name="pre_pool", bufs=PRE_BUFS))
        small = ctx.enter_context(tc.tile_pool(name="small", bufs=PRE_BUFS + 2))
        results = ctx.enter_context(tc.tile_pool(name="results", bufs=5))
        psum_first = ctx.enter_context(tc.psum_pool(name="psum_first", bufs=N_FIRST))
        psum_turn = ctx.enter_context(tc.psum_pool(name="psum_turn", bufs=N_TURN))
        psum_last = ctx.enter_context(tc.psum_pool(name="psum_last", bufs=N_LAST))
        ctx.enter_context(tc.manual_schedule())

        eps = consts.tile([P, 1], F32)
        nc.vector.memset(eps[:], EPS)
        def load_by_feature(queue, vec, name):
            column = consts.tile([P, PACK], BF16, name=name)
            queue.dma_start(out=column[:], in_=vec.rearrange("(m t) -> m t", t=PACK))
            return column

        with nc.allow_non_contiguous_dma(reason="four neighbouring elements of a 512-vector to a partition"):
            u1b_raw = load_by_feature(nc.scalar, U1_b, "u1b_raw")
            u3b_raw = load_by_feature(nc.scalar, U3_b, "u3b_raw")
            ident_f32 = consts.tile([P, P], F32)
            make_identity(nc, ident_f32[:])
            ident_bf16 = consts.tile([P, P], BF16)
            make_identity(nc, ident_bf16[:])
            g1_raw = load_by_feature(nc.gpsimd, ln1_g, "g1_raw")
            b1_raw = load_by_feature(nc.gpsimd, ln1_b, "b1_raw")
            g3_raw = load_by_feature(nc.gpsimd, ln3_g, "g3_raw")
            b3_raw = load_by_feature(nc.gpsimd, ln3_b, "b3_raw")
            alpha_raw = consts.tile([P, 1], BF16)
            nc.gpsimd.dma_start(out=alpha_raw[:], in_=alpha.partition_broadcast(P))
            cb_raw = load_by_feature(nc.gpsimd, C_b, "cb_raw")

        u3_rows = consts.tile([P, PACK, DQ], BF16)
        x_chunks = []
        z_tiles = {}
        for c in range(CHUNKS):
            tiles = slice(CHUNK_START[c], CHUNK_START[c] + CHUNK_TILES[c])
            x_chunk = x_in.tile([P, CHUNK_TILES[c], D], BF16)
            nc.sync.dma_start(out=x_chunk[:], in_=x_view[:, tiles, :])
            x_chunks.append(x_chunk)
            if c == 0:
                w1_codes, w1_plane = load_mx_weight(nc, consts, U1_w_words, U1_w_scales, "w1")
            for before, first, count in Z_LOADS:
                if before == c:
                    z_part = z_in.tile([P, count, DQ], BF16, name="z_part_%d" % first)
                    nc.sync.dma_start(out=z_part[:], in_=z_view[:, first : first + count, :])
                    for i in range(count):
                        z_tiles[first + i] = z_part[:, i, :]
            if c == U3_AT:
                nc.sync.dma_start(out=u3_rows[:], in_=U3_w.rearrange("(m t) k -> m t k", t=PACK))
            if c == C_AT:
                c_codes, c_plane = load_mx_weight(nc, consts, C_w_words, C_w_scales, "c")

        table_warm = consts.tile([P, 1], F32)
        nc.scalar.activation(out=table_warm[:], in_=eps[:], func=ACT.Abs_reciprocal_sqrt)

        first_row = consts.tile([P, P], BF16)
        nc.vector.memset(first_row[:], 0.0)
        nc.vector.memset(first_row[0:1, :], 1.0)

        xq_codes = keep.tile([P, TOKENS], U32, align_bytes=64)
        xq_plane = keep.tile([P, TOKENS], U8, align_bytes=64)
        z2T = keep.tile([P, TOKENS], BF16)
        grouped_x = {}

        def chunk_columns(c):
            return slice(P * CHUNK_START[c], P * (CHUNK_START[c] + CHUNK_TILES[c]))

        def unpack(c):
            n_tiles = CHUNK_TILES[c]
            x_words = x_chunks[c][:].rearrange("p i d -> p (i d)").bitcast(F32)
            words_per_tile = D // 2
            x_grouped = x_stage.tile([P, 4 * P, PACK], BF16, align_bytes=64)
            grouped_words = x_grouped[:].rearrange("p w t -> p (w t)").bitcast(F32)
            for half in range(n_tiles // 2):
                pool, tag = (psum_last, "last") if XPOOL[c] else (psum_turn, "turn")
                xT_bank = pool.tile([P, 2, 2, P], F32, tag=tag)
                for i in range(2):
                    first = words_per_tile * (2 * half + i)
                    for u in range(2):
                        nc.tensor.transpose(
                            xT_bank[:, i, u, :],
                            x_words[:, first + u : first + words_per_tile : 2],
                            ident_f32[:],
                        )
                copy = nc.vector.tensor_copy if half < X_ON_VECTOR[c] else nc.scalar.copy
                copy(
                    out=grouped_words[:, 4 * P * half : 4 * P * (half + 1)].rearrange(
                        "p (i w u) -> p i w u", i=2, u=2
                    ),
                    in_=xT_bank[:].rearrange("p i u w -> p i w u"),
                )
            grouped_x[c] = x_grouped
            pool, tag = (psum_last, "last") if ZPOOL[c] else (psum_turn, "turn")
            zT_bank = pool.tile([P, n_tiles, P], BF16, tag=tag)
            for i in range(n_tiles):
                nc.tensor.transpose(zT_bank[:, i, :], z_tiles[CHUNK_START[c] + i], ident_bf16[:])
            nc.scalar.copy(out=z2T[:, chunk_columns(c)], in_=zT_bank[:].rearrange("p i w -> p (i w)"))

        def quantise_x(c):
            nc.vector.quantize_mx(
                out=xq_codes[:, chunk_columns(c)].bitcast(FP8X4),
                scales=xq_plane[:, chunk_columns(c)],
                in_=grouped_x[c][:, 0 : P * CHUNK_TILES[c], :].rearrange("p w t -> p (w t)"),
            )

        def spread(column, ident, dtype):
            bank = psum_turn.tile([P, PACK, P], dtype, tag="turn")
            for t in range(PACK):
                nc.tensor.transpose(bank[:, t, :], column[:, t : t + 1].to_broadcast([P, P]), ident[:])
            return bank

        u3T = consts.tile([P, PACK, P], BF16)
        bias1 = consts.tile([P, PACK, P], F32)
        bias3 = consts.tile([P, PACK, P], F32)
        bias3_rows = consts.tile([P, PACK, P], BF16)
        bias_out = consts.tile([P, D], F32)
        biases = [bias1, bias3]
        gate_gain = consts.tile([P, PACK], F32)
        gate_shift = consts.tile([P, PACK], F32)
        offset1_spread = consts.tile([P, PACK, P], F32)
        offset1 = consts.tile([P, PACK], F32)

        def constants_of_the_first_matmuls():
            nc.vector.tensor_copy(out=bias1[:], in_=spread(u1b_raw, ident_bf16, BF16)[:])
            u3T_bank = psum_last.tile([P, PACK, P], BF16, tag="last")
            for t in range(PACK):
                nc.tensor.transpose(u3T_bank[:, t, :], u3_rows[:, t, :], ident_bf16[:])
            nc.vector.tensor_copy(out=u3T[:], in_=u3T_bank[:])
            bias3_bank = spread(u3b_raw, ident_bf16, BF16)
            nc.vector.tensor_copy(out=bias3[:], in_=bias3_bank[:])
            nc.vector.tensor_copy(out=bias3_rows[:], in_=bias3_bank[:])

        def spreads_of_the_gate():
            nc.vector.tensor_copy(out=offset1_spread[:], in_=spread(offset1, ident_f32, F32)[:])
            nc.vector.tensor_copy(
                out=bias_out[:].rearrange("p (m t) -> p m t", t=PACK),
                in_=spread(cb_raw, ident_bf16, BF16)[:].rearrange("p t m -> p m t"),
            )

        def constants_of_the_gate():
            alpha_f32 = consts.tile([P, 1], F32)
            nc.gpsimd.tensor_copy(out=alpha_f32[:], in_=alpha_raw[:])
            affine1 = consts.tile([P, 2, PACK], F32)
            nc.gpsimd.tensor_copy(out=affine1[:, 0, :], in_=g1_raw[:])
            nc.gpsimd.tensor_copy(out=affine1[:, 1, :], in_=b1_raw[:])
            gain1, shift1 = affine1[:, 0, :], affine1[:, 1, :]
            gain3 = consts.tile([P, PACK], F32)
            nc.gpsimd.tensor_scalar(
                out=gain3[:], in0=g3_raw[:], scalar1=alpha_f32[:, 0:1], scalar2=None, op0=ALU.mult
            )
            shift3 = consts.tile([P, PACK], F32)
            nc.gpsimd.tensor_scalar(
                out=shift3[:], in0=b3_raw[:], scalar1=alpha_f32[:, 0:1], scalar2=1.0, op0=ALU.mult, op1=ALU.add
            )
            negative = consts.tile([P, 2, PACK], F32)
            nc.vector.tensor_scalar(out=negative[:], in0=affine1[:], scalar1=-1.0, scalar2=None, op0=ALU.mult)
            magnitude = consts.tile([P, 2, PACK], F32)
            nc.vector.tensor_tensor(out=magnitude[:], in0=affine1[:], in1=negative[:], op=ALU.max)
            floor1 = consts.tile([P, PACK], F32)
            nc.vector.tensor_scalar(
                out=floor1[:], in0=magnitude[:, 1, :], scalar1=2.0**-100, scalar2=2.0**-126,
                op0=ALU.mult, op1=ALU.max,
            )
            large_enough = consts.tile([P, PACK], F32)
            nc.vector.tensor_tensor(out=large_enough[:], in0=magnitude[:, 0, :], in1=floor1[:], op=ALU.is_ge)
            safe_gain = consts.tile([P, PACK], F32)
            nc.vector.tensor_tensor(out=safe_gain[:], in0=gain1, in1=floor1[:], op=ALU.subtract)
            nc.vector.tensor_tensor(out=safe_gain[:], in0=safe_gain[:], in1=large_enough[:], op=ALU.mult)
            nc.vector.tensor_tensor(out=safe_gain[:], in0=safe_gain[:], in1=floor1[:], op=ALU.add)
            nc.vector.reciprocal(out=offset1[:], in_=safe_gain[:])
            nc.vector.tensor_tensor(out=offset1[:], in0=offset1[:], in1=shift1, op=ALU.mult)
            nc.gpsimd.tensor_tensor(out=gate_gain[:], in0=safe_gain[:], in1=gain3[:], op=ALU.mult)
            nc.gpsimd.tensor_tensor(out=gate_shift[:], in0=safe_gain[:], in1=shift3[:], op=ALU.mult)

        live = {}

        def group_state(g):
            return live.setdefault(g, {})

        def on_scalar(tile):
            return tile % 2 == 1 and tile >= SCALAR_FROM

        def first_matmul(g, piece):
            j, branch = divmod(piece, 2)
            tile = FIRST_TILE[g] + j
            cols = slice(P * tile, P * (tile + 1))
            acc = psum_first.tile([P, D], F32, tag="first")
            if branch == 0:
                nc.tensor.matmul_mx(
                    out=acc[:],
                    lhsT=xq_codes[:, cols].bitcast(FP8X4),
                    lhsT_scale=xq_plane[:, cols],
                    rhs=w1_codes[:].bitcast(FP8X4),
                    rhs_scale=w1_plane[:],
                    start=True,
                    stop=True,
                )
                by_feature_tile = acc[:].rearrange("p (m t) -> p t m", t=PACK)
            else:
                if on_scalar(tile):
                    nc.tensor.matmul(
                        out=acc[:],
                        lhsT=first_row[:],
                        rhs=bias3_rows[:].rearrange("k t m -> k (t m)"),
                        start=True,
                        stop=False,
                    )
                nc.tensor.matmul(
                    out=acc[:],
                    lhsT=z2T[:, cols],
                    rhs=u3T[:].rearrange("k t m -> k (t m)"),
                    start=not on_scalar(tile),
                    stop=True,
                )
                by_feature_tile = acc[:].rearrange("p (t m) -> p t m", t=PACK)
            group_state(g)[("first", piece)] = by_feature_tile

        def add_first_bias(g, piece):
            j, branch = divmod(piece, 2)
            s = live[g]
            if piece == 0:
                y1 = pre_pool.tile([P, 2, PACK, P], F32)
                y3 = pre_pool.tile([P, 2, PACK, P], F32)
                sums = small.tile([P, 2, 2], F32)
                s["pre_norm"] = [y1, y3]
                s["sums"] = sums
            if branch == 1 and on_scalar(FIRST_TILE[g] + j):
                nc.scalar.activation(
                    out=s["pre_norm"][branch][:, j, :, :],
                    in_=s[("first", piece)],
                    func=ACT.Identity,
                    accum_out=s["sums"][:, branch, j : j + 1],
                )
                return
            nc.vector.scalar_tensor_tensor(
                out=s["pre_norm"][branch][:, j, :, :],
                in0=s[("first", piece)],
                scalar=1.0,
                in1=biases[branch][:],
                op0=ALU.mult,
                op1=ALU.add,
                accum_out=s["sums"][:, branch, j : j + 1],
            )

        def square(g, piece):
            j, branch = divmod(piece, 2)
            s = live[g]
            size = SIZES[g]
            if piece == 0:
                square_sums = small.tile([P, 2, 2], F32)
                s["square_sums"] = square_sums
            squares = stage.tile([P, D], F32)
            nc.scalar.activation(
                out=squares[:],
                in_=s["pre_norm"][branch][:, j, :, :].rearrange("p t m -> p (t m)"),
                func=ACT.Square,
                bias=s["sums"][:, branch, j : j + 1],
                scale=-float(D),
                accum_out=s["square_sums"][:, branch, j : j + 1],
            )

        def reciprocal_deviation(g):
            size = SIZES[g]
            rstd = small.tile([P, 2, 2], F32)
            nc.scalar.activation(
                out=rstd[:, :, 0:size],
                in_=live[g]["square_sums"][:, :, 0:size],
                func=ACT.Abs_reciprocal_sqrt,
                bias=eps[:, 0:1],
                scale=1.0 / D**3,
            )
            live[g]["rstd"] = rstd

        def negative_mean(g):
            size = SIZES[g]
            neg_mean = small.tile([P, 2, 2], F32)
            nc.vector.tensor_scalar(
                out=neg_mean[:, :, 0:size], in0=live[g]["sums"][:, :, 0:size], scalar1=-1.0 / D, scalar2=None, op0=ALU.mult
            )
            live[g]["neg_mean"] = neg_mean

        def normalise(g, piece):
            size = SIZES[g]
            s = live[g]
            branch, j = 1 - piece // size, piece % size
            if piece == 0:
                n1 = normed_pool.tile([P, 2, PACK, P], F32)
                n3 = normed_pool.tile([P, 2, PACK, P], F32)
                s["normed"] = [n1, n3]
            (nc.vector if g == GROUPS - 1 and piece in NORM_V else nc.gpsimd).tensor_scalar(
                out=s["normed"][branch][:, j, :, :],
                in0=s["pre_norm"][branch][:, j, :, :],
                scalar1=s["neg_mean"][:, branch, j : j + 1],
                scalar2=s["rstd"][:, branch, j : j + 1],
                op0=ALU.add,
                op1=ALU.mult,
            )

        def transposes(g, piece):
            size = SIZES[g]
            s = live[g]
            if piece < size:
                nT_bank = psum_turn.tile([P, 4 // size, size * P], F32, tag="turn")
                for k in range(4 // size):
                    for j in range(size):
                        nc.tensor.transpose(
                            nT_bank[:, k, P * j : P * (j + 1)],
                            s["normed"][1][:, j, (4 // size) * piece + k, :],
                            ident_f32[:],
                        )
            else:
                j = piece - size
                nT_bank = psum_turn.tile([P, PACK, P], F32, tag="turn")
                for t in range(PACK):
                    nc.tensor.matmul(
                        out=nT_bank[:, t, :], lhsT=offset1_spread[:, t, :], rhs=ident_f32[:],
                        is_transpose=True, start=True, stop=False,
                    )
                    nc.tensor.matmul(
                        out=nT_bank[:, t, :], lhsT=s["normed"][0][:, j, t, :], rhs=ident_f32[:],
                        is_transpose=True, start=False, stop=True,
                    )
            s[("turned", piece)] = nT_bank

        def gain_and_shift(g, piece):
            size = SIZES[g]
            s = live[g]
            if piece == 0:
                o3T = scaled_pool.tile([P, PACK, 2 * P], F32)
                s["scaled"] = o3T
            for k in range(4 // size):
                t = (4 // size) * piece + k
                nc.scalar.activation(
                    out=s["scaled"][:, t, 0 : P * size],
                    in_=s[("turned", piece)][:, k, :],
                    func=ACT.Identity,
                    bias=gate_shift[:, t : t + 1],
                    scale=gate_gain[:, t : t + 1],
                )

        def gate(g, j):
            s = live[g]
            if j == 0:
                h_grouped = normed_pool.tile([P, 2 * P, PACK], BF16, align_bytes=64)
                s["h_grouped"] = h_grouped
            nc.vector.tensor_tensor(
                out=s["h_grouped"][:, P * j : P * (j + 1), :].rearrange("p (c i) t -> p c t i", i=8),
                in0=s[("turned", SIZES[g] + j)][:].rearrange("p t (c i) -> p c t i", i=8),
                in1=s["scaled"][:, :, P * j : P * (j + 1)].rearrange("p t (c i) -> p c t i", i=8),
                op=ALU.mult,
            )

        def quantise_h(g, first, count):
            if first == 0:
                hq_codes = normed_pool.tile([P, 2 * P], U32, align_bytes=64)
                hq_plane = normed_pool.tile([P, 2 * P], U8, align_bytes=64)
                live[g]["hq"] = (hq_codes, hq_plane)
            hq_codes, hq_plane = live[g]["hq"]
            cols = slice(P * first, P * (first + count))
            nc.vector.quantize_mx(
                out=hq_codes[:, cols].bitcast(FP8X4),
                scales=hq_plane[:, cols],
                in_=live[g]["h_grouped"][:, cols, :].rearrange("p w t -> p (w t)"),
            )

        def last_matmul(g, j):
            hq_codes, hq_plane = live[g]["hq"]
            acc_out = psum_last.tile([P, D], F32, tag="last")
            nc.tensor.matmul_mx(
                out=acc_out[:],
                lhsT=hq_codes[:, P * j : P * (j + 1)].bitcast(FP8X4),
                lhsT_scale=hq_plane[:, P * j : P * (j + 1)],
                rhs=c_codes[:].bitcast(FP8X4),
                rhs_scale=c_plane[:],
                start=True,
                stop=True,
            )
            live[g][("last", j)] = acc_out

        def add_last_bias(g, j):
            result = results.tile([P, D], F32)
            nc.vector.tensor_tensor(out=result[:], in0=live[g][("last", j)][:], in1=bias_out[:], op=ALU.add)
            nc.sync.dma_start(out=out_view[:, FIRST_TILE[g] + j, :], in_=result[:])

        events = []

        def at(slot, rank, step, *arguments):
            events.append((slot, rank, len(events), step, arguments))

        for g in range(GROUPS):
            size, start = SIZES[g], START[g]
            final = g == GROUPS - 1
            late = g >= GROUPS - LATE
            for j in range(size):
                at(start + GATE[size] + j, 1, gate, g, j)
                if late:
                    at(start + LAST_LATE + j * LSTEP, LRANK, last_matmul, g, j)
                    at(start + ADD_LATE + j * LSTEP, ARANK, add_last_bias, g, j)
                else:
                    at(start + LAST[size] + j, 12, last_matmul, g, j)
                    at(start + ADD[size], 2, add_last_bias, g, j)
                if final and QSPLIT:
                    at(start + GATE[size] + j, 1.5, quantise_h, g, j, 1)
            if not (final and QSPLIT):
                at(start + QH[size], 4, quantise_h, g, 0, size)
            at(start + NRM[size], 5, negative_mean, g)
            at(start + SQ[size] + 2 * size - 1, RRANK, reciprocal_deviation, g)
            for piece in range(2 * size):
                at(start + piece - AHEAD_F, 11, first_matmul, g, piece)
                at(start + piece, 6, add_first_bias, g, piece)
                at(start + SQ[size] + piece, 7, square, g, piece)
                at(start + (NRM[size] if not final else NRM_FINAL) + piece * (1 if not final else NSTEP), 9, normalise, g, piece)
                at(start + TRN[size] + piece, 10, transposes, g, piece)
            for piece in range(size):
                at(start + EV[size] + piece, 8, gain_and_shift, g, piece)
        for c in range(CHUNKS):
            at(UNPACK_SLOT[c], 13, unpack, c)
            at(UNPACK_SLOT[c] + QX_LAG, 3, quantise_x, c)
        at(CONST_A_SLOT, 14, constants_of_the_first_matmuls)
        at(CONST_B_SLOT, 14, constants_of_the_gate)
        at(CONST_C_SLOT, 14, spreads_of_the_gate)
        for event in sorted(events, key=lambda e: e[:3]):
            event[3](*event[4])
